import numpy as np
import ml_dtypes


def mxq(x, axis, fmt="e4m3"):
    dtype, down = {"e4m3": (ml_dtypes.float8_e4m3fn, 7), "e5m2": (ml_dtypes.float8_e5m2, 14)}[fmt]
    v = np.moveaxis(np.asarray(x, np.float32).astype(ml_dtypes.bfloat16).astype(np.float64), axis, -1)
    blocks = v.reshape(v.shape[:-1] + (-1, 32))
    amax = np.abs(blocks).max(-1, keepdims=True)
    byte = np.maximum(np.where(amax > 0, np.frexp(amax)[1] - 1 + 127, 0) - down, 1)
    scale = np.exp2(byte - 127.0)
    codes = (blocks / scale).astype(np.float32).astype(dtype).astype(np.float64)
    return np.moveaxis((codes * scale).reshape(v.shape), -1, axis)


WIDE = False


def mx_kscale(k):
    if not WIDE:
        return np.ones(k)
    levels = np.array([10, -10, 5, -5, 0])
    if k % 512:
        return np.exp2(np.random.permutation(np.resize(levels, k // 32))).repeat(32)
    a = np.empty((k // 512, 16))
    for p in range(k // 512):
        a[p, :8] = np.random.permutation(np.resize(levels, 8))
        for g in range(8):
            far = levels[np.abs(levels - a[p, g]) >= 10]
            a[p, g + 8] = far[np.random.randint(len(far))]
    return np.exp2(a.ravel()).repeat(32)


BF16 = ml_dtypes.bfloat16


def bf(x):
    return np.asarray(x, np.float32).astype(BF16)


def f64(x):
    return np.asarray(x).astype(np.float64)


M, N, E, P, S, B, KT = 512, 512, 4, 32, 17, 4096, 2


def setup_inputs():
    s = mx_kscale(M)
    return {
        "z": bf(np.random.standard_normal((M, B)) * s[:, None]),
        "mlp_out": bf(np.random.standard_normal((B, E)) * 0.65),
        "t2": bf(0.5 + 0.1 * np.random.random_sample(1)),
        "A": bf(np.random.standard_normal((E, M)) * 0.5 / s),
        "W": bf(np.random.standard_normal((E, M, M)) / np.sqrt(M) / s),
        "h": bf(np.random.standard_normal((E, M)) * 0.1),
    }


def reference(z, mlp_out, t2, A, W, h):
    z = f64(z)
    lg = -f64(mlp_out).T / f64(t2)[0]
    ex = np.exp(lg - lg.max(axis=0, keepdims=True))
    w_exp = ex / ex.sum(axis=0, keepdims=True)
    zcat = np.concatenate([z[:-P], np.maximum(z[-P:], 0.0)], axis=0)
    Az = f64(A)[:, :, None] * z[None, :, :]
    Wz = mxq(f64(W), 2, "e4m3") @ mxq(zcat, 0, "e4m3")
    expert_out = Az + Wz + f64(h)[:, :, None]
    return np.sum(expert_out * w_exp[:, None, :], axis=0)

@@ -1,0 +1,339 @@
+from contextlib import ExitStack
+
+import concourse.mybir as mybir
+from concourse.masks import make_identity
+
+F32 = mybir.dt.float32
+BF16 = mybir.dt.bfloat16
+I32 = mybir.dt.int32
+U32 = mybir.dt.uint32
+U8 = mybir.dt.uint8
+FP8X4 = mybir.dt.float8_e4m3fn_x4
+ALU = mybir.AluOpType
+ACT = mybir.ActivationFunctionType
+AX = mybir.AxisListType
+
+P = 128
+M = 512
+B = 4096
+E = 4
+NT = B // P
+GW = 512
+NG = B // GW
+TPG = GW // P
+MT = M // P
+OFF_TILES = [0, 1, 2, 2, 2, 2, 2, 2]
+LAG = 4
+AHEAD_COPY = 4
+AHEAD_QUANT = 3
+FIELD_BUFS = 10
+BANKS = 8
+
+FLOPS = 2 * E * M * M * B
+
+
+def tile_dynamix_pb_t_kernel(tc, z, mlp_out, t2, A, W, h, out):
+    nc = tc.nc
+    with ExitStack() as ctx:
+        ctx.enter_context(tc.manual_schedule())
+        keep = ctx.enter_context(tc.tile_pool(name="keep", bufs=1))
+        stage = ctx.enter_context(tc.tile_pool(name="stage", bufs=2))
+        zstage = ctx.enter_context(tc.tile_pool(name="zstage", bufs=6))
+        fields = ctx.enter_context(tc.tile_pool(name="fields", bufs=FIELD_BUFS))
+        outs = ctx.enter_context(tc.tile_pool(name="outs", bufs=6))
+        psum = ctx.enter_context(tc.psum_pool(name="psum", bufs=1))
+        bank_uses = []
+
+        def bank(shape, dtype):
+            n = len(bank_uses)
+            bank_uses.append(n)
+            return psum.tile(shape, dtype, tag="bank%d" % (n % BANKS), name="use%d" % n)
+
+        z_raw = keep.tile([P, MT, B], BF16, name="z_raw")
+        zq = keep.tile([P, B], U32, name="zq", align_bytes=64)
+        zs = keep.tile([P, B], U8, name="zs", align_bytes=64)
+        w_raw = keep.tile([P, E * MT, M], BF16, name="w_raw")
+        wq = keep.tile([P, E, M], U32, name="wq", align_bytes=64)
+        ws = keep.tile([P, E, M], U8, name="ws", align_bytes=64)
+        gate_rows = keep.tile([P, B], BF16, name="gate_rows")
+        gate_pad = keep.tile([P, NT, P], BF16, name="gate_pad")
+        a_raw = keep.tile([P, M], BF16, name="a_raw")
+        h_raw = keep.tile([P, M], BF16, name="h_raw")
+        a_pad = keep.tile([P, M], BF16, name="a_pad")
+        h_pad = keep.tile([P, M], BF16, name="h_pad")
+        last_block = keep.tile([P, 1], F32, name="last_block")
+        floor = keep.tile([P, 1], F32, name="floor")
+        h_bc = keep.tile([P, E, M], BF16, name="h_bc")
+        dh = keep.tile([P, E - 1, M], F32, name="dh")
+        h_col = keep.tile([P, MT], F32, name="h_col")
+        ident_f = keep.tile([P, P], F32, name="ident_f")
+        ident_b = keep.tile([P, P], BF16, name="ident_b")
+        warm = keep.tile([P, 1], F32, name="warm")
+        ml_rows = keep.tile([P, P * E], BF16, name="ml_rows")
+        t2b = keep.tile([P, 1], BF16, name="t2b")
+        t2f = keep.tile([P, 1], F32, name="t2f")
+        rinv = keep.tile([P, 1], F32, name="rinv")
+        lg = keep.tile([P, NT, E], F32, name="lg")
+        mx = keep.tile([P, NT], F32, name="mx")
+        ex = keep.tile([P, NT, E], F32, name="ex")
+        sm = keep.tile([P, NT], F32, name="sm")
+        rs = keep.tile([P, NT], F32, name="rs")
+        gate = keep.tile([P, NT, E], F32, name="gate")
+        g3m1 = keep.tile([P, NT], F32, name="g3m1")
+
+        z_view = z.rearrange("(p j) b -> p j b", j=MT)
+        out_view = out.rearrange("(p j) b -> p j b", j=MT)
+
+        def load_z(g):
+            gs = slice(GW * g, GW * (g + 1))
+            nc.sync.dma_start(out=z_raw[:, :, gs], in_=z_view[:, :, gs])
+
+        nc.scalar.dma_start(out=ml_rows[0:NT, :], in_=mlp_out.rearrange("(t p) e -> t (p e)", p=P))
+        with nc.allow_non_contiguous_dma(reason="one value to every partition"):
+            nc.scalar.dma_start(out=t2b[:], in_=t2.partition_broadcast(P))
+        for e in range(E):
+            nc.sync.dma_start(
+                out=w_raw[:, MT * e:MT * (e + 1), :],
+                in_=W[e].rearrange("(p j) k -> p j k", j=MT),
+            )
+        load_z(0)
+        load_z(1)
+        nc.sync.dma_start(out=h_bc[:].rearrange("p e m -> p (e m)"),
+                          in_=h.rearrange("e m -> (e m)").partition_broadcast(P))
+        for g in range(2, NG):
+            load_z(g)
+
+        nc.vector.memset(ml_rows[32:64, :].bitcast(I32), 0)
+        nc.vector.memset(ml_rows[64:128, :].bitcast(I32), 0)
+        nc.vector.memset(warm[:], 0.0)
+        nc.scalar.activation(out=warm[:], in_=warm[:], func=ACT.Exp)
+        nc.vector.memset(a_raw[:].bitcast(I32), 0)
+        nc.vector.memset(h_raw[:].bitcast(I32), 0)
+        nc.vector.memset(gate_pad[:].rearrange("p t c -> p (t c)").bitcast(I32), 0)
+        make_identity(nc, ident_b[:])
+        make_identity(nc, ident_f[:])
+        for part in range(2):
+            nc.scalar.dma_start(out=a_raw[E * part:E * (part + 1), :], in_=A)
+            nc.scalar.dma_start(out=h_raw[E * part:E * part + 3, :], in_=h[0:3, :])
+            nc.scalar.dma_start(out=h_raw[8 + part:9 + part, :], in_=h[3:4, :])
+        nc.gpsimd.tensor_copy(out=h_pad[:].rearrange("q (j r) -> q j r", j=MT),
+                              in_=h_raw[:].rearrange("q (r j) -> q j r", j=MT))
+        nc.gpsimd.tensor_copy(out=a_pad[:].rearrange("q (j r) -> q j r", j=MT),
+                              in_=a_raw[:].rearrange("q (r j) -> q j r", j=MT))
+        nc.vector.tensor_reduce(out=last_block[:], in_=ident_f[:, P - 8:P], axis=AX.X, op=ALU.add)
+        nc.vector.tensor_scalar(out=floor[:], in0=last_block[:], scalar1=-1.0, scalar2=3.4e38,
+                                op0=ALU.add, op1=ALU.mult)
+
+        z_grouped = {}
+
+        def relu_rows(tb):
+            zr = z_grouped[tb][96:128, :, :].rearrange("p b t -> p (b t)")
+            nc.vector.tensor_scalar(out=zr, in0=zr, scalar1=floor[96:128, 0:1], scalar2=None, op0=ALU.max)
+
+        def regroup_z(tb):
+            cs = slice(P * tb, P * (tb + 1))
+            zg = zstage.tile([P, P, 4], BF16, tag="zg", align_bytes=64)
+            nc.scalar.copy(
+                out=zg[:].rearrange("p (c i) t -> p c t i", i=4),
+                in_=z_raw[:, :, cs].rearrange("p t (c i) -> p c t i", i=4),
+            )
+            z_grouped[tb] = zg
+
+        def quantise_z(tb):
+            cs = slice(P * tb, P * (tb + 1))
+            nc.vector.quantize_mx(out=zq[:, cs].bitcast(FP8X4), scales=zs[:, cs],
+                                  in_=z_grouped[tb][:].rearrange("p b t -> p (b t)"))
+
+        def softmax_first():
+            nc.vector.tensor_copy(out=t2f[:], in_=t2b[:])
+            nc.vector.reciprocal(out=rinv[:], in_=t2f[:])
+            nc.vector.tensor_scalar(out=lg[:], in0=ml_cols[:, :, 0:NT].rearrange("p e t -> p t e"),
+                                    scalar1=rinv[:, 0:1], scalar2=-1.0, op0=ALU.mult, op1=ALU.mult)
+            nc.vector.tensor_reduce(out=mx[:], in_=lg[:], axis=AX.X, op=ALU.max)
+            nc.vector.tensor_tensor(out=lg[:], in0=lg[:], in1=mx[:].unsqueeze(2).to_broadcast([P, NT, E]),
+                                    op=ALU.subtract)
+            nc.scalar.activation(out=ex[:], in_=lg[:], func=ACT.Exp)
+
+        def softmax_second():
+            nc.vector.tensor_reduce(out=sm[:], in_=ex[:], axis=AX.X, op=ALU.add)
+            nc.vector.reciprocal(out=rs[:], in_=sm[:])
+            nc.vector.tensor_tensor(out=gate[:], in0=ex[:], in1=rs[:].unsqueeze(2).to_broadcast([P, NT, E]),
+                                    op=ALU.mult)
+
+        def gate_parts():
+            nc.vector.tensor_copy(out=gate_pad[:, :, 0:E], in_=gate[:])
+            nc.vector.tensor_tensor(out=gate_pad[:, :, E:2 * E], in0=gate[:], in1=gate_pad[:, :, 0:E],
+                                    op=ALU.subtract)
+            nc.vector.tensor_scalar_add(out=g3m1[:], in0=gate[:, :, 3], scalar1=-1.0)
+            nc.vector.tensor_copy(out=gate_pad[:, :, 8], in_=g3m1[:])
+            nc.vector.tensor_tensor(out=gate_pad[:, :, 9], in0=g3m1[:], in1=gate_pad[:, :, 8], op=ALU.subtract)
+
+        ml_cols = bank([P, E, P], BF16)
+        for e in range(E):
+            nc.tensor.transpose(ml_cols[:, e, :], ml_rows[:].rearrange("t (p e) -> t e p", e=E)[:, e, :], ident_b[:])
+
+        w_banks = {}
+        w_grouped = {}
+        for e in range(E):
+            w_grouped[e] = keep.tile([P, M, 4], BF16, name="wg%d" % e, align_bytes=64)
+            for half in range(2):
+                xt = bank([P, 2, 2, P], F32)
+                for a in range(2):
+                    words = w_raw[:, MT * e + 2 * half + a, :].bitcast(F32)
+                    for u in range(2):
+                        nc.tensor.transpose(xt[:, a, u, :], words[:, u:M // 2:2], ident_f[:])
+                w_banks[(e, half)] = xt
+
+        def w_exit(e, half, on_vector):
+            dst = (w_grouped[e][:, 256 * half:256 * (half + 1), :].rearrange("p m j -> p (m j)").bitcast(F32)
+                   .rearrange("p (a r u) -> p a r u", a=2, u=2))
+            src = w_banks[(e, half)][:].rearrange("p a u r -> p a r u")
+            if on_vector:
+                nc.vector.tensor_copy(out=dst, in_=src)
+            else:
+                nc.scalar.copy(out=dst, in_=src)
+
+        def w_quantise(e):
+            nc.vector.quantize_mx(out=wq[:, e, :].bitcast(FP8X4), scales=ws[:, e, :],
+                                  in_=w_grouped[e][:].rearrange("p m j -> p (m j)"))
+
+        w_exit(0, 1, True)
+        w_exit(0, 0, False)
+        w_exit(1, 0, True)
+        w_exit(1, 1, False)
+        w_quantise(0)
+        w_exit(2, 1, False)
+        softmax_first()
+        w_exit(2, 0, True)
+        w_quantise(1)
+        regroup_z(0)
+        w_quantise(2)
+        regroup_z(1)
+        relu_rows(0)
+        softmax_second()
+        w_exit(3, 0, False)
+        quantise_z(0)
+        regroup_z(2)
+        relu_rows(1)
+        w_exit(3, 1, True)
+        quantise_z(1)
+        w_quantise(3)
+
+        def gate_quarter(q):
+            wt = bank([P, 8, P], BF16)
+            for i in range(8):
+                nc.tensor.transpose(wt[:, i, :], gate_pad[:, 8 * q + i, :], ident_b[:])
+            nc.vector.tensor_copy(out=gate_rows[:, 1024 * q:1024 * (q + 1)],
+                                  in_=wt[:].rearrange("p t c -> p (t c)"))
+
+        def h3_column():
+            ht = bank([P, MT, P], BF16)
+            for mt in range(MT):
+                nc.tensor.transpose(ht[:, mt, :], h_pad[:, P * mt:P * (mt + 1)], ident_b[:])
+            nc.vector.tensor_copy(out=h_col[:], in_=ht[:, :, 8])
+
+        for e in range(E - 1):
+            nc.gpsimd.tensor_tensor(out=dh[:, e, :].rearrange("p (j r) -> p j r", j=MT),
+                                    in0=h_bc[:, e, :].rearrange("p (r j) -> p j r", j=MT),
+                                    in1=h_bc[:, 3, :].rearrange("p (r j) -> p j r", j=MT), op=ALU.subtract)
+        off_tiles = [TPG * g + i for g in range(NG) for i in range(TPG - OFF_TILES[g], TPG)]
+        product_fields = {}
+        for tb in off_tiles:
+            gh = keep.tile([P, M], F32, name="gh%d" % tb)
+            nc.gpsimd.tensor_scalar(out=gh[:], in0=dh[:, 0, :], scalar1=gate[:, tb, 0:1], scalar2=0.0,
+                                    op0=ALU.mult, op1=ALU.add)
+            for e in range(1, E - 1):
+                tm = stage.tile([P, M], F32, tag="tm")
+                nc.gpsimd.tensor_scalar(out=tm[:], in0=dh[:, e, :], scalar1=gate[:, tb, e:e + 1], scalar2=0.0,
+                                        op0=ALU.mult, op1=ALU.add)
+                nc.gpsimd.tensor_tensor(out=gh[:], in0=gh[:], in1=tm[:], op=ALU.add)
+            product_fields[tb] = [gh]
+
+        banks = {}
+        tile_fields = {}
+        unit_banks = {}
+        unit_out = {}
+
+        def mx_pass(tb, e):
+            bs = slice(P * tb, P * (tb + 1))
+            pe = bank([P, M], F32)
+            nc.tensor.matmul_mx(out=pe[:], lhsT=zq[:, bs].bitcast(FP8X4), lhsT_scale=zs[:, bs],
+                                rhs=wq[:, e, :].bitcast(FP8X4), rhs_scale=ws[:, e, :],
+                                start=True, stop=True)
+            banks[(tb, e)] = pe
+
+        def scalar_exit(tb, e):
+            fld = fields.tile([P, M], F32, tag="f%d" % (e // 2))
+            nc.scalar.activation(out=fld[:], in_=banks[(tb, e)][:], func=ACT.Copy, scale=gate[:, tb, e:e + 1])
+            tile_fields[tb] = tile_fields.get(tb, []) + [fld]
+
+        def vector_exit(tb, e):
+            fld = tile_fields[tb][e // 2]
+            nc.vector.scalar_tensor_tensor(out=fld[:], in0=banks[(tb, e)][:], scalar=gate[:, tb, e:e + 1],
+                                           in1=fld[:], op0=ALU.mult, op1=ALU.add)
+
+        def plain_part(u):
+            g, mt = u // MT, u % MT
+            gs = slice(GW * g, GW * (g + 1))
+            ms = slice(P * mt, P * (mt + 1))
+            wide = GW - P * OFF_TILES[g]
+            todo = [(i, fld) for i in range(TPG)
+                    for fld in tile_fields[TPG * g + i] + product_fields.get(TPG * g + i, [])]
+            b2 = bank([P, GW], F32)
+            nc.tensor.matmul(out=b2[:], lhsT=a_pad[:, ms], rhs=gate_rows[:, gs], start=True, stop=True)
+            b1 = bank([P, GW], F32)
+            nc.tensor.matmul(out=b1[:, 0:wide], lhsT=h_pad[:, ms],
+                             rhs=gate_rows[:, GW * g:GW * g + wide], start=True, stop=False)
+            for n, (i, fld) in enumerate(todo):
+                nc.tensor.matmul(out=b1[:, P * i:P * (i + 1)], lhsT=fld[:, ms], rhs=ident_f[:],
+                                 is_transpose=True, start=False, stop=(n == len(todo) - 1))
+            unit_banks[u] = (b2, b1)
+
+        def times_z(u):
+            g, mt = u // MT, u % MT
+            xs = outs.tile([P, GW], F32, tag="xs")
+            nc.vector.tensor_tensor(out=xs[:], in0=unit_banks[u][0][:],
+                                    in1=z_raw[:, mt, GW * g:GW * (g + 1)], op=ALU.mult)
+            unit_out[u] = xs
+
+        def last_add(u):
+            g, mt = u // MT, u % MT
+            xs = unit_out[u]
+            nc.vector.scalar_tensor_tensor(out=xs[:], in0=unit_banks[u][1][:], scalar=h_col[:, mt:mt + 1],
+                                           in1=xs[:], op0=ALU.add, op1=ALU.add)
+            nc.sync.dma_start(out=out_view[:, mt, GW * g:GW * (g + 1)], in_=xs[:])
+
+        UNITS = NG * MT
+        for s in range(-1, NT + LAG + 1):
+            u = s - LAG
+            for e_scalar, e_vector in ((0, 1), (2, 3)):
+                if s + 1 < NT:
+                    mx_pass(s + 1, e_scalar)
+                if 0 <= s < NT:
+                    mx_pass(s, e_vector)
+            if 0 <= u < UNITS:
+                plain_part(u)
+            if s + 1 < NT:
+                scalar_exit(s + 1, 0)
+                scalar_exit(s + 1, 2)
+            nxt = s + AHEAD_COPY
+            if nxt < NT:
+                regroup_z(nxt)
+            if s + AHEAD_QUANT < NT:
+                relu_rows(s + AHEAD_QUANT)
+            if 0 <= u - 1 < UNITS:
+                last_add(u - 1)
+            if 0 <= s < NT:
+                vector_exit(s, 1)
+                vector_exit(s, 3)
+            if 0 <= u < UNITS:
+                times_z(u)
+            if s == -1:
+                gate_parts()
+            if s == 0:
+                gate_quarter(0)
+                h3_column()
+            if 1 <= s <= 3:
+                gate_quarter(s)
+            if s + AHEAD_QUANT < NT:
+                quantise_z(s + AHEAD_QUANT)

@@ -24,8 +24,7 @@ TPG = GW // P
 MT = M // P
 OFF_TILES = [0, 1, 2, 2, 2, 2, 2, 2]
 LAG = 4
-AHEAD_COPY = 4
-AHEAD_QUANT = 3
+AHEAD_COPY = 8
 FIELD_BUFS = 10
 BANKS = 8
 
@@ -38,7 +37,7 @@ def tile_dynamix_pb_t_kernel(tc, z, mlp_out, t2, A, W, h, out):
         ctx.enter_context(tc.manual_schedule())
         keep = ctx.enter_context(tc.tile_pool(name="keep", bufs=1))
         stage = ctx.enter_context(tc.tile_pool(name="stage", bufs=2))
-        zstage = ctx.enter_context(tc.tile_pool(name="zstage", bufs=6))
+        zstage = ctx.enter_context(tc.tile_pool(name="zstage", bufs=4))
         fields = ctx.enter_context(tc.tile_pool(name="fields", bufs=FIELD_BUFS))
         outs = ctx.enter_context(tc.tile_pool(name="outs", bufs=6))
         psum = ctx.enter_context(tc.psum_pool(name="psum", bufs=1))
@@ -126,23 +125,25 @@ def tile_dynamix_pb_t_kernel(tc, z, mlp_out, t2, A, W, h, out):
 
         z_grouped = {}
 
-        def relu_rows(tb):
-            zr = z_grouped[tb][96:128, :, :].rearrange("p b t -> p (b t)")
+        def relu_rows(tb, tiles):
+            zr = z_grouped[tb // TPG][96:128, P * (tb % TPG):P * (tb % TPG + tiles), :].rearrange("p b t -> p (b t)")
             nc.vector.tensor_scalar(out=zr, in0=zr, scalar1=floor[96:128, 0:1], scalar2=None, op0=ALU.max)
 
         def regroup_z(tb):
             cs = slice(P * tb, P * (tb + 1))
-            zg = zstage.tile([P, P, 4], BF16, tag="zg", align_bytes=64)
+            if tb % TPG == 0:
+                zg = zstage.tile([P, GW, 4], BF16, tag="zg", align_bytes=64)
+                z_grouped[tb // TPG] = zg
             nc.scalar.copy(
-                out=zg[:].rearrange("p (c i) t -> p c t i", i=4),
+                out=z_grouped[tb // TPG][:, P * (tb % TPG):P * (tb % TPG + 1), :].rearrange("p (c i) t -> p c t i", i=4),
                 in_=z_raw[:, :, cs].rearrange("p t (c i) -> p c t i", i=4),
             )
-            z_grouped[tb] = zg
 
-        def quantise_z(tb):
-            cs = slice(P * tb, P * (tb + 1))
+        def quantise_z(tb, tiles):
+            cs = slice(P * tb, P * (tb + tiles))
             nc.vector.quantize_mx(out=zq[:, cs].bitcast(FP8X4), scales=zs[:, cs],
-                                  in_=z_grouped[tb][:].rearrange("p b t -> p (b t)"))
+                                  in_=z_grouped[tb // TPG][:, P * (tb % TPG):P * (tb % TPG + tiles), :]
+                                  .rearrange("p b t -> p (b t)"))
 
         def softmax_first():
             nc.vector.tensor_copy(out=t2f[:], in_=t2b[:])
@@ -209,14 +210,14 @@ def tile_dynamix_pb_t_kernel(tc, z, mlp_out, t2, A, W, h, out):
         regroup_z(0)
         w_quantise(2)
         regroup_z(1)
-        relu_rows(0)
+        relu_rows(0, 1)
         softmax_second()
         w_exit(3, 0, False)
-        quantise_z(0)
+        quantise_z(0, 1)
         regroup_z(2)
-        relu_rows(1)
+        relu_rows(1, 1)
         w_exit(3, 1, True)
-        quantise_z(1)
+        quantise_z(1, 1)
         w_quantise(3)
 
         def gate_quarter(q):
@@ -304,6 +305,7 @@ def tile_dynamix_pb_t_kernel(tc, z, mlp_out, t2, A, W, h, out):
             nc.sync.dma_start(out=out_view[:, mt, GW * g:GW * (g + 1)], in_=xs[:])
 
         UNITS = NG * MT
+        regrouped = [2]
         for s in range(-1, NT + LAG + 1):
             u = s - LAG
             for e_scalar, e_vector in ((0, 1), (2, 3)):
@@ -316,13 +318,15 @@ def tile_dynamix_pb_t_kernel(tc, z, mlp_out, t2, A, W, h, out):
             if s + 1 < NT:
                 scalar_exit(s + 1, 0)
                 scalar_exit(s + 1, 2)
-            nxt = s + AHEAD_COPY
-            if nxt < NT:
-                regroup_z(nxt)
-            if s + AHEAD_QUANT < NT:
-                relu_rows(s + AHEAD_QUANT)
+            while regrouped[0] < min(NT - 1, s + AHEAD_COPY, 2 * s + 5):
+                regrouped[0] += 1
+                regroup_z(regrouped[0])
+            if s < 1:
+                relu_rows(s + 3, 1)
             if 0 <= u - 1 < UNITS:
                 last_add(u - 1)
+            if s > 0 and (s + 2) % TPG == 0 and s + 2 < NT:
+                quantise_z(s + 2, TPG)
             if 0 <= s < NT:
                 vector_exit(s, 1)
                 vector_exit(s, 3)
@@ -335,5 +339,7 @@ def tile_dynamix_pb_t_kernel(tc, z, mlp_out, t2, A, W, h, out):
                 h3_column()
             if 1 <= s <= 3:
                 gate_quarter(s)
-            if s + AHEAD_QUANT < NT:
-                quantise_z(s + AHEAD_QUANT)
+            if s < 1:
+                quantise_z(s + 3, 1)
+            if (s + 3) % TPG == 0 and s + 3 < NT:
+                relu_rows(s + 3, TPG)

@@ -24,7 +24,9 @@ TPG = GW // P
 MT = M // P
 OFF_TILES = [0, 1, 2, 2, 2, 2, 2, 2]
 LAG = 4
-AHEAD_COPY = 8
+AHEAD_COPY = 9
+QLEAD = 3
+PROD_BUFS = 12
 FIELD_BUFS = 10
 BANKS = 8
 
@@ -36,7 +38,7 @@ def tile_dynamix_pb_t_kernel(tc, z, mlp_out, t2, A, W, h, out):
     with ExitStack() as ctx:
         ctx.enter_context(tc.manual_schedule())
         keep = ctx.enter_context(tc.tile_pool(name="keep", bufs=1))
-        stage = ctx.enter_context(tc.tile_pool(name="stage", bufs=2))
+        products = ctx.enter_context(tc.tile_pool(name="products", bufs=PROD_BUFS))
         zstage = ctx.enter_context(tc.tile_pool(name="zstage", bufs=4))
         fields = ctx.enter_context(tc.tile_pool(name="fields", bufs=FIELD_BUFS))
         outs = ctx.enter_context(tc.tile_pool(name="outs", bufs=6))
@@ -239,16 +241,11 @@ def tile_dynamix_pb_t_kernel(tc, z, mlp_out, t2, A, W, h, out):
                                     in1=h_bc[:, 3, :].rearrange("p (r j) -> p j r", j=MT), op=ALU.subtract)
         off_tiles = [TPG * g + i for g in range(NG) for i in range(TPG - OFF_TILES[g], TPG)]
         product_fields = {}
-        for tb in off_tiles:
-            gh = keep.tile([P, M], F32, name="gh%d" % tb)
-            nc.gpsimd.tensor_scalar(out=gh[:], in0=dh[:, 0, :], scalar1=gate[:, tb, 0:1], scalar2=0.0,
-                                    op0=ALU.mult, op1=ALU.add)
-            for e in range(1, E - 1):
-                tm = stage.tile([P, M], F32, tag="tm")
-                nc.gpsimd.tensor_scalar(out=tm[:], in0=dh[:, e, :], scalar1=gate[:, tb, e:e + 1], scalar2=0.0,
-                                        op0=ALU.mult, op1=ALU.add)
-                nc.gpsimd.tensor_tensor(out=gh[:], in0=gh[:], in1=tm[:], op=ALU.add)
-            product_fields[tb] = [gh]
+
+        def h_product(tb, e):
+            pf = products.tile([P, M], F32, tag="pf")
+            nc.scalar.activation(out=pf[:], in_=dh[:, e, :], func=ACT.Copy, scale=gate[:, tb, e:e + 1])
+            product_fields[tb] = product_fields.get(tb, []) + [pf]
 
         banks = {}
         tile_fields = {}
@@ -318,15 +315,19 @@ def tile_dynamix_pb_t_kernel(tc, z, mlp_out, t2, A, W, h, out):
             if s + 1 < NT:
                 scalar_exit(s + 1, 0)
                 scalar_exit(s + 1, 2)
-            while regrouped[0] < min(NT - 1, s + AHEAD_COPY, 2 * s + 5):
+            if 0 <= s < NT:
+                todo_h = [(tb, e) for tb in off_tiles if tb // TPG == s // TPG for e in range(E - 1)]
+                for tb, e in todo_h[len(todo_h) * (s % TPG) // TPG:len(todo_h) * (s % TPG + 1) // TPG]:
+                    h_product(tb, e)
+            while regrouped[0] < min(NT - 1, s + AHEAD_COPY, 3 * s + 7):
                 regrouped[0] += 1
                 regroup_z(regrouped[0])
             if s < 1:
                 relu_rows(s + 3, 1)
             if 0 <= u - 1 < UNITS:
                 last_add(u - 1)
-            if s > 0 and (s + 2) % TPG == 0 and s + 2 < NT:
-                quantise_z(s + 2, TPG)
+            if s > 0 and (s + QLEAD) % TPG == 0 and s + QLEAD < NT:
+                quantise_z(s + QLEAD, TPG)
             if 0 <= s < NT:
                 vector_exit(s, 1)
                 vector_exit(s, 3)
@@ -341,5 +342,5 @@ def tile_dynamix_pb_t_kernel(tc, z, mlp_out, t2, A, W, h, out):
                 gate_quarter(s)
             if s < 1:
                 quantise_z(s + 3, 1)
-            if (s + 3) % TPG == 0 and s + 3 < NT:
-                relu_rows(s + 3, TPG)
+            if s > -1 and (s + QLEAD + 1) % TPG == 0 and s + QLEAD + 1 < NT:
+                relu_rows(s + QLEAD + 1, TPG)

@@ -92,12 +92,14 @@ def tile_dynamix_pb_t_kernel(tc, z, mlp_out, t2, A, W, h, out):
         nc.scalar.dma_start(out=ml_rows[0:NT, :], in_=mlp_out.rearrange("(t p) e -> t (p e)", p=P))
         with nc.allow_non_contiguous_dma(reason="one value to every partition"):
             nc.scalar.dma_start(out=t2b[:], in_=t2.partition_broadcast(P))
-        for e in range(E):
-            nc.sync.dma_start(
-                out=w_raw[:, MT * e:MT * (e + 1), :],
-                in_=W[e].rearrange("(p j) k -> p j k", j=MT),
-            )
+        def load_w(e):
+            nc.sync.dma_start(out=w_raw[:, MT * e:MT * (e + 1), :], in_=W[e].rearrange("(p j) k -> p j k", j=MT))
+
+        load_w(0)
+        load_w(1)
         load_z(0)
+        load_w(2)
+        load_w(3)
         load_z(1)
         nc.sync.dma_start(out=h_bc[:].rearrange("p e m -> p (e m)"),
                           in_=h.rearrange("e m -> (e m)").partition_broadcast(P))
@@ -141,6 +143,15 @@ def tile_dynamix_pb_t_kernel(tc, z, mlp_out, t2, A, W, h, out):
                 in_=z_raw[:, :, cs].rearrange("p t (c i) -> p c t i", i=4),
             )
 
+        def regroup_relu_z(tb):
+            cs = slice(P * tb, P * (tb + 1))
+            if tb % TPG == 0:
+                zg = zstage.tile([P, GW, 4], BF16, tag="zg", align_bytes=64)
+                z_grouped[tb // TPG] = zg
+            nc.vector.tensor_scalar(out=z_grouped[tb // TPG][:, P * (tb % TPG):P * (tb % TPG + 1), :],
+                                    in0=z_raw[:, :, cs].rearrange("p t c -> p c t"),
+                                    scalar1=floor[:, 0:1], scalar2=None, op0=ALU.max)
+
         def quantise_z(tb, tiles):
             cs = slice(P * tb, P * (tb + tiles))
             nc.vector.quantize_mx(out=zq[:, cs].bitcast(FP8X4), scales=zs[:, cs],
@@ -177,7 +188,8 @@ def tile_dynamix_pb_t_kernel(tc, z, mlp_out, t2, A, W, h, out):
 
         w_banks = {}
         w_grouped = {}
-        for e in range(E):
+
+        def w_turn(e):
             w_grouped[e] = keep.tile([P, M, 4], BF16, name="wg%d" % e, align_bytes=64)
             for half in range(2):
                 xt = bank([P, 2, 2, P], F32)
@@ -200,40 +212,45 @@ def tile_dynamix_pb_t_kernel(tc, z, mlp_out, t2, A, W, h, out):
             nc.vector.quantize_mx(out=wq[:, e, :].bitcast(FP8X4), scales=ws[:, e, :],
                                   in_=w_grouped[e][:].rearrange("p m j -> p (m j)"))
 
-        w_exit(0, 1, True)
-        w_exit(0, 0, False)
-        w_exit(1, 0, True)
-        w_exit(1, 1, False)
-        w_quantise(0)
-        w_exit(2, 1, False)
-        softmax_first()
-        w_exit(2, 0, True)
-        w_quantise(1)
-        regroup_z(0)
-        w_quantise(2)
-        regroup_z(1)
-        relu_rows(0, 1)
-        softmax_second()
-        w_exit(3, 0, False)
-        quantise_z(0, 1)
-        regroup_z(2)
-        relu_rows(1, 1)
-        w_exit(3, 1, True)
-        quantise_z(1, 1)
-        w_quantise(3)
-
         def gate_quarter(q):
             wt = bank([P, 8, P], BF16)
             for i in range(8):
                 nc.tensor.transpose(wt[:, i, :], gate_pad[:, 8 * q + i, :], ident_b[:])
-            nc.vector.tensor_copy(out=gate_rows[:, 1024 * q:1024 * (q + 1)],
-                                  in_=wt[:].rearrange("p t c -> p (t c)"))
+            nc.scalar.copy(out=gate_rows[:, 1024 * q:1024 * (q + 1)], in_=wt[:].rearrange("p t c -> p (t c)"))
 
         def h3_column():
             ht = bank([P, MT, P], BF16)
             for mt in range(MT):
                 nc.tensor.transpose(ht[:, mt, :], h_pad[:, P * mt:P * (mt + 1)], ident_b[:])
             nc.vector.tensor_copy(out=h_col[:], in_=ht[:, :, 8])
+
+        softmax_first()
+        softmax_second()
+        gate_parts()
+        w_turn(0)
+        w_turn(1)
+        for e in range(2):
+            w_exit(e, 0, False)
+            w_exit(e, 1, True)
+        for q in range(4):
+            gate_quarter(q)
+        w_quantise(0)
+        regroup_relu_z(0)
+        w_quantise(1)
+        regroup_relu_z(1)
+        regroup_relu_z(2)
+        quantise_z(0, 2)
+        regroup_relu_z(3)
+        w_turn(2)
+        w_turn(3)
+        w_exit(2, 0, False)
+        w_exit(2, 1, True)
+        quantise_z(2, 2)
+        w_exit(3, 0, False)
+        w_exit(3, 1, True)
+        w_quantise(2)
+        h3_column()
+        w_quantise(3)
 
         for e in range(E - 1):
             nc.gpsimd.tensor_tensor(out=dh[:, e, :].rearrange("p (j r) -> p j r", j=MT),
@@ -261,12 +278,12 @@ def tile_dynamix_pb_t_kernel(tc, z, mlp_out, t2, A, W, h, out):
             banks[(tb, e)] = pe
 
         def scalar_exit(tb, e):
-            fld = fields.tile([P, M], F32, tag="f%d" % (e // 2))
+            fld = fields.tile([P, M], F32, tag="f%d" % e)
             nc.scalar.activation(out=fld[:], in_=banks[(tb, e)][:], func=ACT.Copy, scale=gate[:, tb, e:e + 1])
             tile_fields[tb] = tile_fields.get(tb, []) + [fld]
 
         def vector_exit(tb, e):
-            fld = tile_fields[tb][e // 2]
+            fld = tile_fields[tb][e - 2]
             nc.vector.scalar_tensor_tensor(out=fld[:], in0=banks[(tb, e)][:], scalar=gate[:, tb, e:e + 1],
                                            in1=fld[:], op0=ALU.mult, op1=ALU.add)
 
@@ -302,10 +319,10 @@ def tile_dynamix_pb_t_kernel(tc, z, mlp_out, t2, A, W, h, out):
             nc.sync.dma_start(out=out_view[:, mt, GW * g:GW * (g + 1)], in_=xs[:])
 
         UNITS = NG * MT
-        regrouped = [2]
+        regrouped = [7]
         for s in range(-1, NT + LAG + 1):
             u = s - LAG
-            for e_scalar, e_vector in ((0, 1), (2, 3)):
+            for e_scalar, e_vector in ((0, 2), (1, 3)):
                 if s + 1 < NT:
                     mx_pass(s + 1, e_scalar)
                 if 0 <= s < NT:
@@ -314,33 +331,25 @@ def tile_dynamix_pb_t_kernel(tc, z, mlp_out, t2, A, W, h, out):
                 plain_part(u)
             if s + 1 < NT:
                 scalar_exit(s + 1, 0)
-                scalar_exit(s + 1, 2)
+                scalar_exit(s + 1, 1)
             if 0 <= s < NT:
                 todo_h = [(tb, e) for tb in off_tiles if tb // TPG == s // TPG for e in range(E - 1)]
                 for tb, e in todo_h[len(todo_h) * (s % TPG) // TPG:len(todo_h) * (s % TPG + 1) // TPG]:
                     h_product(tb, e)
-            while regrouped[0] < min(NT - 1, s + AHEAD_COPY, 3 * s + 7):
+            while regrouped[0] < min(NT - 1, s + AHEAD_COPY, 2 * s + 9):
                 regrouped[0] += 1
                 regroup_z(regrouped[0])
             if s < 1:
-                relu_rows(s + 3, 1)
+                regroup_relu_z(2 * s + 6)
+                regroup_relu_z(2 * s + 7)
             if 0 <= u - 1 < UNITS:
                 last_add(u - 1)
             if s > 0 and (s + QLEAD) % TPG == 0 and s + QLEAD < NT:
                 quantise_z(s + QLEAD, TPG)
             if 0 <= s < NT:
-                vector_exit(s, 1)
+                vector_exit(s, 2)
                 vector_exit(s, 3)
             if 0 <= u < UNITS:
                 times_z(u)
-            if s == -1:
-                gate_parts()
-            if s == 0:
-                gate_quarter(0)
-                h3_column()
-            if 1 <= s <= 3:
-                gate_quarter(s)
-            if s < 1:
-                quantise_z(s + 3, 1)
-            if s > -1 and (s + QLEAD + 1) % TPG == 0 and s + QLEAD + 1 < NT:
+            if s > 0 and (s + QLEAD + 1) % TPG == 0 and s + QLEAD + 1 < NT:
                 relu_rows(s + QLEAD + 1, TPG)

@@ -342,14 +342,17 @@ def tile_dynamix_pb_t_kernel(tc, z, mlp_out, t2, A, W, h, out):
             if s < 1:
                 regroup_relu_z(2 * s + 6)
                 regroup_relu_z(2 * s + 7)
+            if 0 <= s < NT:
+                vector_exit(s, 2)
+            if s >= NT and 0 <= u < UNITS:
+                times_z(u)
             if 0 <= u - 1 < UNITS:
                 last_add(u - 1)
             if s > 0 and (s + QLEAD) % TPG == 0 and s + QLEAD < NT:
                 quantise_z(s + QLEAD, TPG)
             if 0 <= s < NT:
-                vector_exit(s, 2)
                 vector_exit(s, 3)
-            if 0 <= u < UNITS:
+            if s < NT and 0 <= u < UNITS:
                 times_z(u)
             if s > 0 and (s + QLEAD + 1) % TPG == 0 and s + QLEAD + 1 < NT:
                 relu_rows(s + QLEAD + 1, TPG)

@@ -139,8 +139,8 @@ def tile_dynamix_pb_t_kernel(tc, z, mlp_out, t2, A, W, h, out):
                 zg = zstage.tile([P, GW, 4], BF16, tag="zg", align_bytes=64)
                 z_grouped[tb // TPG] = zg
             nc.scalar.copy(
-                out=z_grouped[tb // TPG][:, P * (tb % TPG):P * (tb % TPG + 1), :].rearrange("p (c i) t -> p c t i", i=4),
-                in_=z_raw[:, :, cs].rearrange("p t (c i) -> p c t i", i=4),
+                out=z_grouped[tb // TPG][:, P * (tb % TPG):P * (tb % TPG + 1), :],
+                in_=z_raw[:, :, cs].rearrange("p t c -> p c t"),
             )
 
         def regroup_relu_z(tb):

@@ -26,7 +26,9 @@ OFF_TILES = [0, 1, 2, 2, 2, 2, 2, 2]
 LAG = 4
 AHEAD_COPY = 9
 QLEAD = 3
-PROD_BUFS = 12
+VECTOR_GROUPS = 2
+PROD_BUFS = 4
+H_BUFS = 6
 FIELD_BUFS = 10
 BANKS = 8
 
@@ -62,6 +64,7 @@ def tile_dynamix_pb_t_kernel(tc, z, mlp_out, t2, A, W, h, out):
         h_raw = keep.tile([P, M], BF16, name="h_raw")
         a_pad = keep.tile([P, M], BF16, name="a_pad")
         h_pad = keep.tile([P, M], BF16, name="h_pad")
+        z_last = keep.tile([P, B // 4], BF16, name="z_last")
         last_block = keep.tile([P, 1], F32, name="last_block")
         floor = keep.tile([P, 1], F32, name="floor")
         h_bc = keep.tile([P, E, M], BF16, name="h_bc")
@@ -85,9 +88,24 @@ def tile_dynamix_pb_t_kernel(tc, z, mlp_out, t2, A, W, h, out):
         z_view = z.rearrange("(p j) b -> p j b", j=MT)
         out_view = out.rearrange("(p j) b -> p j b", j=MT)
 
+        RELU_P = P - 8
+        parked = out.bitcast(BF16)[0:P, 2 * (B - GW):2 * B]
+        parked_rows = parked.rearrange("(q j c) n -> q j c n", j=MT, c=4)
+
         def load_z(g):
             gs = slice(GW * g, GW * (g + 1))
-            nc.sync.dma_start(out=z_raw[:, :, gs], in_=z_view[:, :, gs])
+            rows = P if g < VECTOR_GROUPS else RELU_P
+            nc.sync.dma_start(out=z_raw[0:rows, :, gs], in_=z_view[0:rows, :, gs])
+
+        def load_relu_rows(g):
+            gs = slice(GW * g, GW * (g + 1))
+            nc.sync.dma_start(out=z_raw[RELU_P:P, :, gs], in_=parked_rows[:, :, g // 2, GW * (g % 2):GW * (g % 2 + 1)])
+
+        def reload_last_rows(g):
+            gs = slice(GW * g, GW * (g + 1))
+            nc.scalar.dma_start(out=z_raw[RELU_P:P, :, gs], in_=z_view[RELU_P:P, :, gs])
+
+        nc.sync.dma_start(out=z_last[:], in_=z[M - 32:M, :].rearrange("r (c n) -> (r c) n", c=4))
 
         nc.scalar.dma_start(out=ml_rows[0:NT, :], in_=mlp_out.rearrange("(t p) e -> t (p e)", p=P))
         with nc.allow_non_contiguous_dma(reason="one value to every partition"):
@@ -101,37 +119,28 @@ def tile_dynamix_pb_t_kernel(tc, z, mlp_out, t2, A, W, h, out):
         load_w(2)
         load_w(3)
         load_z(1)
+        load_z(2)
         nc.sync.dma_start(out=h_bc[:].rearrange("p e m -> p (e m)"),
                           in_=h.rearrange("e m -> (e m)").partition_broadcast(P))
-        for g in range(2, NG):
-            load_z(g)
 
         nc.vector.memset(ml_rows[32:64, :].bitcast(I32), 0)
         nc.vector.memset(ml_rows[64:128, :].bitcast(I32), 0)
         nc.vector.memset(warm[:], 0.0)
         nc.scalar.activation(out=warm[:], in_=warm[:], func=ACT.Exp)
-        nc.vector.memset(a_raw[:].bitcast(I32), 0)
-        nc.vector.memset(h_raw[:].bitcast(I32), 0)
         nc.vector.memset(gate_pad[:].rearrange("p t c -> p (t c)").bitcast(I32), 0)
         make_identity(nc, ident_b[:])
         make_identity(nc, ident_f[:])
+        nc.gpsimd.memset(a_raw[:], 0.0)
+        nc.gpsimd.memset(h_raw[:], 0.0)
         for part in range(2):
-            nc.scalar.dma_start(out=a_raw[E * part:E * (part + 1), :], in_=A)
-            nc.scalar.dma_start(out=h_raw[E * part:E * part + 3, :], in_=h[0:3, :])
-            nc.scalar.dma_start(out=h_raw[8 + part:9 + part, :], in_=h[3:4, :])
-        nc.gpsimd.tensor_copy(out=h_pad[:].rearrange("q (j r) -> q j r", j=MT),
-                              in_=h_raw[:].rearrange("q (r j) -> q j r", j=MT))
-        nc.gpsimd.tensor_copy(out=a_pad[:].rearrange("q (j r) -> q j r", j=MT),
-                              in_=a_raw[:].rearrange("q (r j) -> q j r", j=MT))
+            nc.gpsimd.dma_start(out=a_raw[E * part:E * (part + 1), :], in_=A)
+            nc.gpsimd.dma_start(out=h_raw[E * part:E * part + 3, :], in_=h[0:3, :])
+            nc.gpsimd.dma_start(out=h_raw[8 + part:9 + part, :], in_=h[3:4, :])
         nc.vector.tensor_reduce(out=last_block[:], in_=ident_f[:, P - 8:P], axis=AX.X, op=ALU.add)
         nc.vector.tensor_scalar(out=floor[:], in0=last_block[:], scalar1=-1.0, scalar2=3.4e38,
                                 op0=ALU.add, op1=ALU.mult)
 
         z_grouped = {}
-
-        def relu_rows(tb, tiles):
-            zr = z_grouped[tb // TPG][96:128, P * (tb % TPG):P * (tb % TPG + tiles), :].rearrange("p b t -> p (b t)")
-            nc.vector.tensor_scalar(out=zr, in0=zr, scalar1=floor[96:128, 0:1], scalar2=None, op0=ALU.max)
 
         def regroup_z(tb):
             cs = slice(P * tb, P * (tb + 1))
@@ -142,6 +151,8 @@ def tile_dynamix_pb_t_kernel(tc, z, mlp_out, t2, A, W, h, out):
                 out=z_grouped[tb // TPG][:, P * (tb % TPG):P * (tb % TPG + 1), :],
                 in_=z_raw[:, :, cs].rearrange("p t c -> p c t"),
             )
+            if tb % TPG == TPG - 1:
+                reload_last_rows(tb // TPG)
 
         def regroup_relu_z(tb):
             cs = slice(P * tb, P * (tb + 1))
@@ -175,12 +186,12 @@ def tile_dynamix_pb_t_kernel(tc, z, mlp_out, t2, A, W, h, out):
                                     op=ALU.mult)
 
         def gate_parts():
-            nc.vector.tensor_copy(out=gate_pad[:, :, 0:E], in_=gate[:])
-            nc.vector.tensor_tensor(out=gate_pad[:, :, E:2 * E], in0=gate[:], in1=gate_pad[:, :, 0:E],
+            nc.gpsimd.tensor_copy(out=gate_pad[:, :, 0:E], in_=gate[:])
+            nc.gpsimd.tensor_tensor(out=gate_pad[:, :, E:2 * E], in0=gate[:], in1=gate_pad[:, :, 0:E],
                                     op=ALU.subtract)
-            nc.vector.tensor_scalar_add(out=g3m1[:], in0=gate[:, :, 3], scalar1=-1.0)
-            nc.vector.tensor_copy(out=gate_pad[:, :, 8], in_=g3m1[:])
-            nc.vector.tensor_tensor(out=gate_pad[:, :, 9], in0=g3m1[:], in1=gate_pad[:, :, 8], op=ALU.subtract)
+            nc.gpsimd.tensor_scalar(out=g3m1[:], in0=gate[:, :, 3], scalar1=-1.0, scalar2=0.0, op0=ALU.add, op1=ALU.add)
+            nc.gpsimd.tensor_copy(out=gate_pad[:, :, 8], in_=g3m1[:])
+            nc.gpsimd.tensor_tensor(out=gate_pad[:, :, 9], in0=g3m1[:], in1=gate_pad[:, :, 8], op=ALU.subtract)
 
         ml_cols = bank([P, E, P], BF16)
         for e in range(E):
@@ -216,7 +227,7 @@ def tile_dynamix_pb_t_kernel(tc, z, mlp_out, t2, A, W, h, out):
             wt = bank([P, 8, P], BF16)
             for i in range(8):
                 nc.tensor.transpose(wt[:, i, :], gate_pad[:, 8 * q + i, :], ident_b[:])
-            nc.scalar.copy(out=gate_rows[:, 1024 * q:1024 * (q + 1)], in_=wt[:].rearrange("p t c -> p (t c)"))
+            nc.vector.tensor_copy(out=gate_rows[:, 1024 * q:1024 * (q + 1)], in_=wt[:].rearrange("p t c -> p (t c)"))
 
         def h3_column():
             ht = bank([P, MT, P], BF16)
@@ -226,14 +237,22 @@ def tile_dynamix_pb_t_kernel(tc, z, mlp_out, t2, A, W, h, out):
 
         softmax_first()
         softmax_second()
+        nc.scalar.activation(out=z_last[:], in_=z_last[:], func=ACT.Relu)
+        nc.scalar.dma_start(out=parked, in_=z_last[:])
+        load_relu_rows(2)
+        for g in range(3, NG):
+            load_z(g)
+            load_relu_rows(g)
         gate_parts()
-        w_turn(0)
-        w_turn(1)
+        nc.gpsimd.tensor_copy(out=h_pad[:].rearrange("q (j r) -> q j r", j=MT),
+                              in_=h_raw[:].rearrange("q (r j) -> q j r", j=MT))
+        nc.gpsimd.tensor_copy(out=a_pad[:].rearrange("q (j r) -> q j r", j=MT),
+                              in_=a_raw[:].rearrange("q (r j) -> q j r", j=MT))
+        for e in range(E):
+            w_turn(e)
         for e in range(2):
             w_exit(e, 0, False)
-            w_exit(e, 1, True)
-        for q in range(4):
-            gate_quarter(q)
+            w_exit(e, 1, False)
         w_quantise(0)
         regroup_relu_z(0)
         w_quantise(1)
@@ -241,15 +260,12 @@ def tile_dynamix_pb_t_kernel(tc, z, mlp_out, t2, A, W, h, out):
         regroup_relu_z(2)
         quantise_z(0, 2)
         regroup_relu_z(3)
-        w_turn(2)
-        w_turn(3)
         w_exit(2, 0, False)
-        w_exit(2, 1, True)
+        w_exit(2, 1, False)
         quantise_z(2, 2)
         w_exit(3, 0, False)
-        w_exit(3, 1, True)
+        w_exit(3, 1, False)
         w_quantise(2)
-        h3_column()
         w_quantise(3)
 
         for e in range(E - 1):
@@ -260,9 +276,15 @@ def tile_dynamix_pb_t_kernel(tc, z, mlp_out, t2, A, W, h, out):
         product_fields = {}
 
         def h_product(tb, e):
-            pf = products.tile([P, M], F32, tag="pf")
-            nc.scalar.activation(out=pf[:], in_=dh[:, e, :], func=ACT.Copy, scale=gate[:, tb, e:e + 1])
-            product_fields[tb] = product_fields.get(tb, []) + [pf]
+            if e == 0:
+                hf = products.tile([P, M], F32, tag="hf", bufs=H_BUFS)
+                nc.scalar.activation(out=hf[:], in_=dh[:, e, :], func=ACT.Copy, scale=gate[:, tb, e:e + 1])
+                product_fields[tb] = [hf]
+            else:
+                pf = products.tile([P, M], F32, tag="pf")
+                nc.scalar.activation(out=pf[:], in_=dh[:, e, :], func=ACT.Copy, scale=gate[:, tb, e:e + 1])
+                hf = product_fields[tb][0]
+                nc.gpsimd.tensor_tensor(out=hf[:], in0=hf[:], in1=pf[:], op=ALU.add)
 
         banks = {}
         tile_fields = {}
@@ -333,7 +355,7 @@ def tile_dynamix_pb_t_kernel(tc, z, mlp_out, t2, A, W, h, out):
                 scalar_exit(s + 1, 0)
                 scalar_exit(s + 1, 1)
             if 0 <= s < NT:
-                todo_h = [(tb, e) for tb in off_tiles if tb // TPG == s // TPG for e in range(E - 1)]
+                todo_h = [(tb, e) for tb in off_tiles if tb // TPG == s // TPG + 1 for e in range(E - 1)]
                 for tb, e in todo_h[len(todo_h) * (s % TPG) // TPG:len(todo_h) * (s % TPG + 1) // TPG]:
                     h_product(tb, e)
             while regrouped[0] < min(NT - 1, s + AHEAD_COPY, 2 * s + 9):
@@ -354,5 +376,7 @@ def tile_dynamix_pb_t_kernel(tc, z, mlp_out, t2, A, W, h, out):
                 vector_exit(s, 3)
             if s < NT and 0 <= u < UNITS:
                 times_z(u)
-            if s > 0 and (s + QLEAD + 1) % TPG == 0 and s + QLEAD + 1 < NT:
-                relu_rows(s + QLEAD + 1, TPG)
+            if 0 <= s < 4:
+                gate_quarter(s)
+            if s == 3:
+                h3_column()

@@ -309,6 +309,11 @@ def tile_dynamix_pb_t_kernel(tc, z, mlp_out, t2, A, W, h, out):
             nc.vector.scalar_tensor_tensor(out=fld[:], in0=banks[(tb, e)][:], scalar=gate[:, tb, e:e + 1],
                                            in1=fld[:], op0=ALU.mult, op1=ALU.add)
 
+        def sum_fields(tb):
+            f0, f1 = tile_fields[tb]
+            nc.gpsimd.tensor_tensor(out=f0[:], in0=f0[:], in1=f1[:], op=ALU.add)
+            tile_fields[tb] = [f0]
+
         def plain_part(u):
             g, mt = u // MT, u % MT
             gs = slice(GW * g, GW * (g + 1))
@@ -374,6 +379,8 @@ def tile_dynamix_pb_t_kernel(tc, z, mlp_out, t2, A, W, h, out):
                 quantise_z(s + QLEAD, TPG)
             if 0 <= s < NT:
                 vector_exit(s, 3)
+                if s % TPG < TPG - 1:
+                    sum_fields(s)
             if s < NT and 0 <= u < UNITS:
                 times_z(u)
             if 0 <= s < 4:

@@ -22,13 +22,20 @@ GW = 512
 NG = B // GW
 TPG = GW // P
 MT = M // P
-OFF_TILES = [0, 1, 2, 2, 2, 2, 2, 2]
 LAG = 4
-AHEAD_COPY = 9
+AHEAD_COPY = 10
+
+
+def products_by(s):
+    return s + max(0, s + AHEAD_COPY + 1 - NT)
+
+
+LEFT_OUT = [products_by(TPG * g + 2) // (E - 1) for g in range(NG)]
+OFF_TILES = [LEFT_OUT[g] - (LEFT_OUT[g - 1] if g > 0 else 0) for g in range(NG)]
 QLEAD = 3
-VECTOR_GROUPS = 2
+VECTOR_GROUPS = 3
 PROD_BUFS = 4
-H_BUFS = 6
+H_BUFS = 8
 FIELD_BUFS = 10
 BANKS = 8
 
@@ -235,14 +242,16 @@ def tile_dynamix_pb_t_kernel(tc, z, mlp_out, t2, A, W, h, out):
                 nc.tensor.transpose(ht[:, mt, :], h_pad[:, P * mt:P * (mt + 1)], ident_b[:])
             nc.vector.tensor_copy(out=h_col[:], in_=ht[:, :, 8])
 
-        softmax_first()
-        softmax_second()
         nc.scalar.activation(out=z_last[:], in_=z_last[:], func=ACT.Relu)
         nc.scalar.dma_start(out=parked, in_=z_last[:])
-        load_relu_rows(2)
-        for g in range(3, NG):
-            load_z(g)
+        load_z(VECTOR_GROUPS)
+        load_z(VECTOR_GROUPS + 1)
+        for g in range(VECTOR_GROUPS, NG):
             load_relu_rows(g)
+            if g + 2 < NG:
+                load_z(g + 2)
+        softmax_first()
+        softmax_second()
         gate_parts()
         nc.gpsimd.tensor_copy(out=h_pad[:].rearrange("q (j r) -> q j r", j=MT),
                               in_=h_raw[:].rearrange("q (r j) -> q j r", j=MT))
@@ -346,7 +355,7 @@ def tile_dynamix_pb_t_kernel(tc, z, mlp_out, t2, A, W, h, out):
             nc.sync.dma_start(out=out_view[:, mt, GW * g:GW * (g + 1)], in_=xs[:])
 
         UNITS = NG * MT
-        regrouped = [7]
+        regrouped = [TPG * VECTOR_GROUPS - 1]
         for s in range(-1, NT + LAG + 1):
             u = s - LAG
             for e_scalar, e_vector in ((0, 2), (1, 3)):
@@ -359,14 +368,13 @@ def tile_dynamix_pb_t_kernel(tc, z, mlp_out, t2, A, W, h, out):
             if s + 1 < NT:
                 scalar_exit(s + 1, 0)
                 scalar_exit(s + 1, 1)
-            if 0 <= s < NT:
-                todo_h = [(tb, e) for tb in off_tiles if tb // TPG == s // TPG + 1 for e in range(E - 1)]
-                for tb, e in todo_h[len(todo_h) * (s % TPG) // TPG:len(todo_h) * (s % TPG + 1) // TPG]:
-                    h_product(tb, e)
+            if 0 < s < NT:
+                for n in range(products_by(s - 1), min(products_by(s), (E - 1) * len(off_tiles))):
+                    h_product(off_tiles[n // (E - 1)], n % (E - 1))
             while regrouped[0] < min(NT - 1, s + AHEAD_COPY, 2 * s + 9):
                 regrouped[0] += 1
                 regroup_z(regrouped[0])
-            if s < 1:
+            if s < 2 * VECTOR_GROUPS - 3:
                 regroup_relu_z(2 * s + 6)
                 regroup_relu_z(2 * s + 7)
             if 0 <= s < NT:
@@ -379,7 +387,7 @@ def tile_dynamix_pb_t_kernel(tc, z, mlp_out, t2, A, W, h, out):
                 quantise_z(s + QLEAD, TPG)
             if 0 <= s < NT:
                 vector_exit(s, 3)
-                if s % TPG < TPG - 1:
+                if s % TPG < 2 and s < NT - TPG:
                     sum_fields(s)
             if s < NT and 0 <= u < UNITS:
                 times_z(u)

@@ -74,9 +74,10 @@ def tile_dynamix_pb_t_kernel(tc, z, mlp_out, t2, A, W, h, out):
         z_last = keep.tile([P, B // 4], BF16, name="z_last")
         last_block = keep.tile([P, 1], F32, name="last_block")
         floor = keep.tile([P, 1], F32, name="floor")
-        h_bc = keep.tile([P, E, M], BF16, name="h_bc")
+        h_sb = keep.tile([P, E, MT], BF16, name="h_sb")
+        h_f = keep.tile([P, E, MT], F32, name="h_f")
+        dh_col = keep.tile([P, E - 1, MT], F32, name="dh_col")
         dh = keep.tile([P, E - 1, M], F32, name="dh")
-        h_col = keep.tile([P, MT], F32, name="h_col")
         ident_f = keep.tile([P, P], F32, name="ident_f")
         ident_b = keep.tile([P, P], BF16, name="ident_b")
         warm = keep.tile([P, 1], F32, name="warm")
@@ -117,6 +118,7 @@ def tile_dynamix_pb_t_kernel(tc, z, mlp_out, t2, A, W, h, out):
         nc.scalar.dma_start(out=ml_rows[0:NT, :], in_=mlp_out.rearrange("(t p) e -> t (p e)", p=P))
         with nc.allow_non_contiguous_dma(reason="one value to every partition"):
             nc.scalar.dma_start(out=t2b[:], in_=t2.partition_broadcast(P))
+            nc.scalar.dma_start(out=h_sb[:], in_=h.rearrange("e (p j) -> p e j", j=MT))
         def load_w(e):
             nc.sync.dma_start(out=w_raw[:, MT * e:MT * (e + 1), :], in_=W[e].rearrange("(p j) k -> p j k", j=MT))
 
@@ -127,8 +129,6 @@ def tile_dynamix_pb_t_kernel(tc, z, mlp_out, t2, A, W, h, out):
         load_w(3)
         load_z(1)
         load_z(2)
-        nc.sync.dma_start(out=h_bc[:].rearrange("p e m -> p (e m)"),
-                          in_=h.rearrange("e m -> (e m)").partition_broadcast(P))
 
         nc.vector.memset(ml_rows[32:64, :].bitcast(I32), 0)
         nc.vector.memset(ml_rows[64:128, :].bitcast(I32), 0)
@@ -236,20 +236,11 @@ def tile_dynamix_pb_t_kernel(tc, z, mlp_out, t2, A, W, h, out):
                 nc.tensor.transpose(wt[:, i, :], gate_pad[:, 8 * q + i, :], ident_b[:])
             nc.vector.tensor_copy(out=gate_rows[:, 1024 * q:1024 * (q + 1)], in_=wt[:].rearrange("p t c -> p (t c)"))
 
-        def h3_column():
-            ht = bank([P, MT, P], BF16)
-            for mt in range(MT):
-                nc.tensor.transpose(ht[:, mt, :], h_pad[:, P * mt:P * (mt + 1)], ident_b[:])
-            nc.vector.tensor_copy(out=h_col[:], in_=ht[:, :, 8])
-
         nc.scalar.activation(out=z_last[:], in_=z_last[:], func=ACT.Relu)
         nc.scalar.dma_start(out=parked, in_=z_last[:])
-        load_z(VECTOR_GROUPS)
-        load_z(VECTOR_GROUPS + 1)
         for g in range(VECTOR_GROUPS, NG):
             load_relu_rows(g)
-            if g + 2 < NG:
-                load_z(g + 2)
+            load_z(g)
         softmax_first()
         softmax_second()
         gate_parts()
@@ -257,11 +248,24 @@ def tile_dynamix_pb_t_kernel(tc, z, mlp_out, t2, A, W, h, out):
                               in_=h_raw[:].rearrange("q (r j) -> q j r", j=MT))
         nc.gpsimd.tensor_copy(out=a_pad[:].rearrange("q (j r) -> q j r", j=MT),
                               in_=a_raw[:].rearrange("q (r j) -> q j r", j=MT))
-        for e in range(E):
-            w_turn(e)
+        w_turn(0)
+        w_turn(1)
+        nc.vector.tensor_copy(out=h_f[:], in_=h_sb[:])
+        nc.vector.tensor_tensor(out=dh_col[:], in0=h_f[:, 0:3, :],
+                                in1=h_f[:, 3, :].unsqueeze(1).to_broadcast([P, E - 1, MT]), op=ALU.subtract)
+        dh_banks = []
+        for e in range(E - 1):
+            db = bank([P, MT, P], F32)
+            for j in range(MT):
+                nc.tensor.transpose(db[:, j, :], dh_col[:, e, j:j + 1].to_broadcast([P, P]), ident_f[:])
+            dh_banks.append(db)
         for e in range(2):
             w_exit(e, 0, False)
             w_exit(e, 1, False)
+        w_turn(2)
+        w_turn(3)
+        for e in range(E - 1):
+            nc.scalar.copy(out=dh[:, e, :].rearrange("p (j r) -> p j r", j=MT), in_=dh_banks[e][:])
         w_quantise(0)
         regroup_relu_z(0)
         w_quantise(1)
@@ -277,10 +281,6 @@ def tile_dynamix_pb_t_kernel(tc, z, mlp_out, t2, A, W, h, out):
         w_quantise(2)
         w_quantise(3)
 
-        for e in range(E - 1):
-            nc.gpsimd.tensor_tensor(out=dh[:, e, :].rearrange("p (j r) -> p j r", j=MT),
-                                    in0=h_bc[:, e, :].rearrange("p (r j) -> p j r", j=MT),
-                                    in1=h_bc[:, 3, :].rearrange("p (r j) -> p j r", j=MT), op=ALU.subtract)
         off_tiles = [TPG * g + i for g in range(NG) for i in range(TPG - OFF_TILES[g], TPG)]
         product_fields = {}
 
@@ -350,7 +350,7 @@ def tile_dynamix_pb_t_kernel(tc, z, mlp_out, t2, A, W, h, out):
         def last_add(u):
             g, mt = u // MT, u % MT
             xs = unit_out[u]
-            nc.vector.scalar_tensor_tensor(out=xs[:], in0=unit_banks[u][1][:], scalar=h_col[:, mt:mt + 1],
+            nc.vector.scalar_tensor_tensor(out=xs[:], in0=unit_banks[u][1][:], scalar=h_f[:, 3, mt:mt + 1],
                                            in1=xs[:], op0=ALU.add, op1=ALU.add)
             nc.sync.dma_start(out=out_view[:, mt, GW * g:GW * (g + 1)], in_=xs[:])
 
@@ -393,5 +393,3 @@ def tile_dynamix_pb_t_kernel(tc, z, mlp_out, t2, A, W, h, out):
                 times_z(u)
             if 0 <= s < 4:
                 gate_quarter(s)
-            if s == 3:
-                h3_column()

@@ -22,7 +22,7 @@ GW = 512
 NG = B // GW
 TPG = GW // P
 MT = M // P
-LAG = 4
+LAG = 5
 AHEAD_COPY = 10
 
 
@@ -36,7 +36,7 @@ QLEAD = 3
 VECTOR_GROUPS = 3
 PROD_BUFS = 4
 H_BUFS = 8
-FIELD_BUFS = 10
+FIELD_BUFS = 11
 BANKS = 8
 
 FLOPS = 2 * E * M * M * B
@@ -297,7 +297,8 @@ def tile_dynamix_pb_t_kernel(tc, z, mlp_out, t2, A, W, h, out):
 
         banks = {}
         tile_fields = {}
-        unit_banks = {}
+        g_banks = {}
+        t_banks = {}
         unit_out = {}
 
         def mx_pass(tb, e):
@@ -323,34 +324,38 @@ def tile_dynamix_pb_t_kernel(tc, z, mlp_out, t2, A, W, h, out):
             nc.gpsimd.tensor_tensor(out=f0[:], in0=f0[:], in1=f1[:], op=ALU.add)
             tile_fields[tb] = [f0]
 
-        def plain_part(u):
+        def gate_a(u):
             g, mt = u // MT, u % MT
-            gs = slice(GW * g, GW * (g + 1))
+            b2 = bank([P, GW], F32)
+            nc.tensor.matmul(out=b2[:], lhsT=a_pad[:, P * mt:P * (mt + 1)], rhs=gate_rows[:, GW * g:GW * (g + 1)],
+                             start=True, stop=True)
+            g_banks[u] = b2
+
+        def turned_sum(u):
+            g, mt = u // MT, u % MT
             ms = slice(P * mt, P * (mt + 1))
             wide = GW - P * OFF_TILES[g]
             todo = [(i, fld) for i in range(TPG)
                     for fld in tile_fields[TPG * g + i] + product_fields.get(TPG * g + i, [])]
-            b2 = bank([P, GW], F32)
-            nc.tensor.matmul(out=b2[:], lhsT=a_pad[:, ms], rhs=gate_rows[:, gs], start=True, stop=True)
             b1 = bank([P, GW], F32)
             nc.tensor.matmul(out=b1[:, 0:wide], lhsT=h_pad[:, ms],
                              rhs=gate_rows[:, GW * g:GW * g + wide], start=True, stop=False)
             for n, (i, fld) in enumerate(todo):
                 nc.tensor.matmul(out=b1[:, P * i:P * (i + 1)], lhsT=fld[:, ms], rhs=ident_f[:],
                                  is_transpose=True, start=False, stop=(n == len(todo) - 1))
-            unit_banks[u] = (b2, b1)
+            t_banks[u] = b1
 
         def times_z(u):
             g, mt = u // MT, u % MT
             xs = outs.tile([P, GW], F32, tag="xs")
-            nc.vector.tensor_tensor(out=xs[:], in0=unit_banks[u][0][:],
+            nc.vector.tensor_tensor(out=xs[:], in0=g_banks[u][:],
                                     in1=z_raw[:, mt, GW * g:GW * (g + 1)], op=ALU.mult)
             unit_out[u] = xs
 
         def last_add(u):
             g, mt = u // MT, u % MT
             xs = unit_out[u]
-            nc.vector.scalar_tensor_tensor(out=xs[:], in0=unit_banks[u][1][:], scalar=h_f[:, 3, mt:mt + 1],
+            nc.vector.scalar_tensor_tensor(out=xs[:], in0=t_banks[u][:], scalar=h_f[:, 3, mt:mt + 1],
                                            in1=xs[:], op0=ALU.add, op1=ALU.add)
             nc.sync.dma_start(out=out_view[:, mt, GW * g:GW * (g + 1)], in_=xs[:])
 
@@ -358,13 +363,16 @@ def tile_dynamix_pb_t_kernel(tc, z, mlp_out, t2, A, W, h, out):
         regrouped = [TPG * VECTOR_GROUPS - 1]
         for s in range(-1, NT + LAG + 1):
             u = s - LAG
-            for e_scalar, e_vector in ((0, 2), (1, 3)):
-                if s + 1 < NT:
-                    mx_pass(s + 1, e_scalar)
-                if 0 <= s < NT:
-                    mx_pass(s, e_vector)
+            if 0 <= u + 1 < UNITS:
+                gate_a(u + 1)
+            if s + 1 < NT:
+                mx_pass(s + 1, 0)
+                mx_pass(s + 1, 1)
+            if 0 <= s < NT:
+                mx_pass(s, 2)
+                mx_pass(s, 3)
             if 0 <= u < UNITS:
-                plain_part(u)
+                turned_sum(u)
             if s + 1 < NT:
                 scalar_exit(s + 1, 0)
                 scalar_exit(s + 1, 1)
@@ -377,19 +385,18 @@ def tile_dynamix_pb_t_kernel(tc, z, mlp_out, t2, A, W, h, out):
             if s < 2 * VECTOR_GROUPS - 3:
                 regroup_relu_z(2 * s + 6)
                 regroup_relu_z(2 * s + 7)
-            if 0 <= s < NT:
-                vector_exit(s, 2)
-            if s >= NT and 0 <= u < UNITS:
-                times_z(u)
+            if s >= NT and 0 <= u + 1 < UNITS:
+                times_z(u + 1)
             if 0 <= u - 1 < UNITS:
                 last_add(u - 1)
             if s > 0 and (s + QLEAD) % TPG == 0 and s + QLEAD < NT:
                 quantise_z(s + QLEAD, TPG)
+            if s < NT and 0 <= u + 1 < UNITS:
+                times_z(u + 1)
             if 0 <= s < NT:
+                vector_exit(s, 2)
                 vector_exit(s, 3)
                 if s % TPG < 2 and s < NT - TPG:
                     sum_fields(s)
-            if s < NT and 0 <= u < UNITS:
-                times_z(u)
             if 0 <= s < 4:
                 gate_quarter(s)

@@ -37,6 +37,7 @@ VECTOR_GROUPS = 3
 PROD_BUFS = 4
 H_BUFS = 8
 FIELD_BUFS = 11
+GZ_BUFS = 4
 BANKS = 8
 
 FLOPS = 2 * E * M * M * B
@@ -299,7 +300,7 @@ def tile_dynamix_pb_t_kernel(tc, z, mlp_out, t2, A, W, h, out):
         tile_fields = {}
         g_banks = {}
         t_banks = {}
-        unit_out = {}
+        gate_z = {}
 
         def mx_pass(tb, e):
             bs = slice(P * tb, P * (tb + 1))
@@ -347,16 +348,16 @@ def tile_dynamix_pb_t_kernel(tc, z, mlp_out, t2, A, W, h, out):
 
         def times_z(u):
             g, mt = u // MT, u % MT
-            xs = outs.tile([P, GW], F32, tag="xs")
-            nc.vector.tensor_tensor(out=xs[:], in0=g_banks[u][:],
+            gz = outs.tile([P, GW], F32, tag="gz", bufs=GZ_BUFS)
+            nc.vector.tensor_tensor(out=gz[:], in0=g_banks[u][:],
                                     in1=z_raw[:, mt, GW * g:GW * (g + 1)], op=ALU.mult)
-            unit_out[u] = xs
+            gate_z[u] = gz
 
         def last_add(u):
             g, mt = u // MT, u % MT
-            xs = unit_out[u]
+            xs = outs.tile([P, GW], F32, tag="xs")
             nc.vector.scalar_tensor_tensor(out=xs[:], in0=t_banks[u][:], scalar=h_f[:, 3, mt:mt + 1],
-                                           in1=xs[:], op0=ALU.add, op1=ALU.add)
+                                           in1=gate_z[u][:], op0=ALU.add, op1=ALU.add)
             nc.sync.dma_start(out=out_view[:, mt, GW * g:GW * (g + 1)], in_=xs[:])
 
         UNITS = NG * MT
@@ -385,18 +386,16 @@ def tile_dynamix_pb_t_kernel(tc, z, mlp_out, t2, A, W, h, out):
             if s < 2 * VECTOR_GROUPS - 3:
                 regroup_relu_z(2 * s + 6)
                 regroup_relu_z(2 * s + 7)
-            if s >= NT and 0 <= u + 1 < UNITS:
+            if 0 <= u + 1 < UNITS:
                 times_z(u + 1)
             if 0 <= u - 1 < UNITS:
                 last_add(u - 1)
             if s > 0 and (s + QLEAD) % TPG == 0 and s + QLEAD < NT:
                 quantise_z(s + QLEAD, TPG)
-            if s < NT and 0 <= u + 1 < UNITS:
-                times_z(u + 1)
             if 0 <= s < NT:
                 vector_exit(s, 2)
                 vector_exit(s, 3)
-                if s % TPG < 2 and s < NT - TPG:
+                if s % TPG < 3 and TPG <= s < NT - TPG:
                     sum_fields(s)
             if 0 <= s < 4:
                 gate_quarter(s)

@@ -101,18 +101,18 @@ def tile_dynamix_pb_t_kernel(tc, z, mlp_out, t2, A, W, h, out):
         parked = out.bitcast(BF16)[0:P, 2 * (B - GW):2 * B]
         parked_rows = parked.rearrange("(q j c) n -> q j c n", j=MT, c=4)
 
-        def load_z(g):
-            gs = slice(GW * g, GW * (g + 1))
+        def load_z(g, groups=1):
+            gs = slice(GW * g, GW * (g + groups))
             rows = P if g < VECTOR_GROUPS else RELU_P
             nc.sync.dma_start(out=z_raw[0:rows, :, gs], in_=z_view[0:rows, :, gs])
 
-        def load_relu_rows(g):
-            gs = slice(GW * g, GW * (g + 1))
-            nc.sync.dma_start(out=z_raw[RELU_P:P, :, gs], in_=parked_rows[:, :, g // 2, GW * (g % 2):GW * (g % 2 + 1)])
+        def load_relu_rows(g, groups=1):
+            gs = slice(GW * g, GW * (g + groups))
+            nc.sync.dma_start(out=z_raw[RELU_P:P, :, gs], in_=parked_rows[:, :, g // 2, GW * (g % 2):GW * (g % 2 + groups)])
 
         def reload_last_rows(g):
             gs = slice(GW * g, GW * (g + 1))
-            nc.scalar.dma_start(out=z_raw[RELU_P:P, :, gs], in_=z_view[RELU_P:P, :, gs])
+            nc.sync.dma_start(out=z_raw[RELU_P:P, :, gs], in_=z_view[RELU_P:P, :, gs])
 
         nc.sync.dma_start(out=z_last[:], in_=z[M - 32:M, :].rearrange("r (c n) -> (r c) n", c=4))
 
@@ -235,13 +235,19 @@ def tile_dynamix_pb_t_kernel(tc, z, mlp_out, t2, A, W, h, out):
             wt = bank([P, 8, P], BF16)
             for i in range(8):
                 nc.tensor.transpose(wt[:, i, :], gate_pad[:, 8 * q + i, :], ident_b[:])
-            nc.vector.tensor_copy(out=gate_rows[:, 1024 * q:1024 * (q + 1)], in_=wt[:].rearrange("p t c -> p (t c)"))
+            rows = gate_rows[:, 1024 * q:1024 * (q + 1)]
+            if q == 0:
+                nc.vector.tensor_copy(out=rows, in_=wt[:].rearrange("p t c -> p (t c)"))
+            else:
+                nc.scalar.copy(out=rows, in_=wt[:].rearrange("p t c -> p (t c)"))
 
         nc.scalar.activation(out=z_last[:], in_=z_last[:], func=ACT.Relu)
         nc.scalar.dma_start(out=parked, in_=z_last[:])
-        for g in range(VECTOR_GROUPS, NG):
-            load_relu_rows(g)
-            load_z(g)
+        load_relu_rows(VECTOR_GROUPS)
+        load_z(VECTOR_GROUPS)
+        for g in range(VECTOR_GROUPS + 1, NG, 2):
+            load_relu_rows(g, 2)
+            load_z(g, 2)
         softmax_first()
         softmax_second()
         gate_parts()
@@ -265,7 +271,7 @@ def tile_dynamix_pb_t_kernel(tc, z, mlp_out, t2, A, W, h, out):
             w_exit(e, 1, False)
         w_turn(2)
         w_turn(3)
-        for e in range(E - 1):
+        for e in (0, 1):
             nc.scalar.copy(out=dh[:, e, :].rearrange("p (j r) -> p j r", j=MT), in_=dh_banks[e][:])
         w_quantise(0)
         regroup_relu_z(0)
@@ -279,6 +285,8 @@ def tile_dynamix_pb_t_kernel(tc, z, mlp_out, t2, A, W, h, out):
         quantise_z(2, 2)
         w_exit(3, 0, False)
         w_exit(3, 1, False)
+        for e in (2,):
+            nc.scalar.copy(out=dh[:, e, :].rearrange("p (j r) -> p j r", j=MT), in_=dh_banks[e][:])
         w_quantise(2)
         w_quantise(3)
 
@@ -288,7 +296,11 @@ def tile_dynamix_pb_t_kernel(tc, z, mlp_out, t2, A, W, h, out):
         def h_product(tb, e):
             if e == 0:
                 hf = products.tile([P, M], F32, tag="hf", bufs=H_BUFS)
-                nc.scalar.activation(out=hf[:], in_=dh[:, e, :], func=ACT.Copy, scale=gate[:, tb, e:e + 1])
+                if tb < NT - 2 * TPG:
+                    nc.gpsimd.tensor_scalar(out=hf[:], in0=dh[:, e, :], scalar1=gate[:, tb, e:e + 1], scalar2=0.0,
+                                            op0=ALU.mult, op1=ALU.add)
+                else:
+                    nc.scalar.activation(out=hf[:], in_=dh[:, e, :], func=ACT.Copy, scale=gate[:, tb, e:e + 1])
                 product_fields[tb] = [hf]
             else:
                 pf = products.tile([P, M], F32, tag="pf")
@@ -395,7 +407,7 @@ def tile_dynamix_pb_t_kernel(tc, z, mlp_out, t2, A, W, h, out):
             if 0 <= s < NT:
                 vector_exit(s, 2)
                 vector_exit(s, 3)
-                if s % TPG < 3 and TPG <= s < NT - TPG:
+                if s % TPG < 2 and s < NT - TPG:
                     sum_fields(s)
-            if 0 <= s < 4:
-                gate_quarter(s)
+            if s == 0 or s > 0 and (s + 2) % (2 * TPG) == 0 and s + 2 < NT:
+                gate_quarter((s + 2) // (2 * TPG))

from contextlib import ExitStack

import concourse.mybir as mybir
from concourse.masks import make_identity

F32 = mybir.dt.float32
BF16 = mybir.dt.bfloat16
I32 = mybir.dt.int32
U32 = mybir.dt.uint32
U8 = mybir.dt.uint8
FP8X4 = mybir.dt.float8_e4m3fn_x4
ALU = mybir.AluOpType
ACT = mybir.ActivationFunctionType
AX = mybir.AxisListType

P = 128
M = 512
B = 4096
E = 4
NT = B // P
GW = 512
NG = B // GW
TPG = GW // P
MT = M // P
LAG = 5
AHEAD_COPY = 10


def products_by(s):
    return s + max(0, s + AHEAD_COPY + 1 - NT)


LEFT_OUT = [products_by(TPG * g + 2) // (E - 1) for g in range(NG)]
OFF_TILES = [LEFT_OUT[g] - (LEFT_OUT[g - 1] if g > 0 else 0) for g in range(NG)]
QLEAD = 3
VECTOR_GROUPS = 3
PROD_BUFS = 4
H_BUFS = 8
FIELD_BUFS = 11
GZ_BUFS = 4
BANKS = 8

FLOPS = 2 * E * M * M * B


def tile_dynamix_pb_t_kernel(tc, z, mlp_out, t2, A, W, h, out):
    nc = tc.nc
    with ExitStack() as ctx:
        ctx.enter_context(tc.manual_schedule())
        keep = ctx.enter_context(tc.tile_pool(name="keep", bufs=1))
        products = ctx.enter_context(tc.tile_pool(name="products", bufs=PROD_BUFS))
        zstage = ctx.enter_context(tc.tile_pool(name="zstage", bufs=4))
        fields = ctx.enter_context(tc.tile_pool(name="fields", bufs=FIELD_BUFS))
        outs = ctx.enter_context(tc.tile_pool(name="outs", bufs=6))
        psum = ctx.enter_context(tc.psum_pool(name="psum", bufs=1))
        bank_uses = []

        def bank(shape, dtype):
            n = len(bank_uses)
            bank_uses.append(n)
            return psum.tile(shape, dtype, tag="bank%d" % (n % BANKS), name="use%d" % n)

        z_raw = keep.tile([P, MT, B], BF16, name="z_raw")
        zq = keep.tile([P, B], U32, name="zq", align_bytes=64)
        zs = keep.tile([P, B], U8, name="zs", align_bytes=64)
        w_raw = keep.tile([P, E * MT, M], BF16, name="w_raw")
        wq = keep.tile([P, E, M], U32, name="wq", align_bytes=64)
        ws = keep.tile([P, E, M], U8, name="ws", align_bytes=64)
        gate_rows = keep.tile([P, B], BF16, name="gate_rows")
        gate_pad = keep.tile([P, NT, P], BF16, name="gate_pad")
        a_raw = keep.tile([P, M], BF16, name="a_raw")
        h_raw = keep.tile([P, M], BF16, name="h_raw")
        a_pad = keep.tile([P, M], BF16, name="a_pad")
        h_pad = keep.tile([P, M], BF16, name="h_pad")
        z_last = keep.tile([P, B // 4], BF16, name="z_last")
        last_block = keep.tile([P, 1], F32, name="last_block")
        floor = keep.tile([P, 1], F32, name="floor")
        h_sb = keep.tile([P, E, MT], BF16, name="h_sb")
        h_f = keep.tile([P, E, MT], F32, name="h_f")
        dh_col = keep.tile([P, E - 1, MT], F32, name="dh_col")
        dh = keep.tile([P, E - 1, M], F32, name="dh")
        ident_f = keep.tile([P, P], F32, name="ident_f")
        ident_b = keep.tile([P, P], BF16, name="ident_b")
        warm = keep.tile([P, 1], F32, name="warm")
        ml_rows = keep.tile([P, P * E], BF16, name="ml_rows")
        t2b = keep.tile([P, 1], BF16, name="t2b")
        t2f = keep.tile([P, 1], F32, name="t2f")
        rinv = keep.tile([P, 1], F32, name="rinv")
        lg = keep.tile([P, NT, E], F32, name="lg")
        mx = keep.tile([P, NT], F32, name="mx")
        ex = keep.tile([P, NT, E], F32, name="ex")
        sm = keep.tile([P, NT], F32, name="sm")
        rs = keep.tile([P, NT], F32, name="rs")
        gate = keep.tile([P, NT, E], F32, name="gate")
        g3m1 = keep.tile([P, NT], F32, name="g3m1")

        z_view = z.rearrange("(p j) b -> p j b", j=MT)
        out_view = out.rearrange("(p j) b -> p j b", j=MT)

        RELU_P = P - 8
        parked = out.bitcast(BF16)[0:P, 2 * (B - GW):2 * B]
        parked_rows = parked.rearrange("(q j c) n -> q j c n", j=MT, c=4)

        def load_z(g, groups=1):
            gs = slice(GW * g, GW * (g + groups))
            rows = P if g < VECTOR_GROUPS else RELU_P
            nc.sync.dma_start(out=z_raw[0:rows, :, gs], in_=z_view[0:rows, :, gs])

        def load_relu_rows(g, groups=1):
            gs = slice(GW * g, GW * (g + groups))
            nc.sync.dma_start(out=z_raw[RELU_P:P, :, gs], in_=parked_rows[:, :, g // 2, GW * (g % 2):GW * (g % 2 + groups)])

        def reload_last_rows(g):
            gs = slice(GW * g, GW * (g + 1))
            nc.sync.dma_start(out=z_raw[RELU_P:P, :, gs], in_=z_view[RELU_P:P, :, gs])

        nc.sync.dma_start(out=z_last[:], in_=z[M - 32:M, :].rearrange("r (c n) -> (r c) n", c=4))

        nc.scalar.dma_start(out=ml_rows[0:NT, :], in_=mlp_out.rearrange("(t p) e -> t (p e)", p=P))
        with nc.allow_non_contiguous_dma(reason="one value to every partition"):
            nc.scalar.dma_start(out=t2b[:], in_=t2.partition_broadcast(P))
            nc.scalar.dma_start(out=h_sb[:], in_=h.rearrange("e (p j) -> p e j", j=MT))
        def load_w(e):
            nc.sync.dma_start(out=w_raw[:, MT * e:MT * (e + 1), :], in_=W[e].rearrange("(p j) k -> p j k", j=MT))

        load_w(0)
        load_w(1)
        load_z(0)
        load_w(2)
        load_w(3)
        load_z(1)
        load_z(2)

        nc.vector.memset(ml_rows[32:64, :].bitcast(I32), 0)
        nc.vector.memset(ml_rows[64:128, :].bitcast(I32), 0)
        nc.vector.memset(warm[:], 0.0)
        nc.scalar.activation(out=warm[:], in_=warm[:], func=ACT.Exp)
        nc.vector.memset(gate_pad[:].rearrange("p t c -> p (t c)").bitcast(I32), 0)
        make_identity(nc, ident_b[:])
        make_identity(nc, ident_f[:])
        nc.gpsimd.memset(a_raw[:], 0.0)
        nc.gpsimd.memset(h_raw[:], 0.0)
        for part in range(2):
            nc.gpsimd.dma_start(out=a_raw[E * part:E * (part + 1), :], in_=A)
            nc.gpsimd.dma_start(out=h_raw[E * part:E * part + 3, :], in_=h[0:3, :])
            nc.gpsimd.dma_start(out=h_raw[8 + part:9 + part, :], in_=h[3:4, :])
        nc.vector.tensor_reduce(out=last_block[:], in_=ident_f[:, P - 8:P], axis=AX.X, op=ALU.add)
        nc.vector.tensor_scalar(out=floor[:], in0=last_block[:], scalar1=-1.0, scalar2=3.4e38,
                                op0=ALU.add, op1=ALU.mult)

        z_grouped = {}

        def regroup_z(tb):
            cs = slice(P * tb, P * (tb + 1))
            if tb % TPG == 0:
                zg = zstage.tile([P, GW, 4], BF16, tag="zg", align_bytes=64)
                z_grouped[tb // TPG] = zg
            nc.scalar.copy(
                out=z_grouped[tb // TPG][:, P * (tb % TPG):P * (tb % TPG + 1), :],
                in_=z_raw[:, :, cs].rearrange("p t c -> p c t"),
            )
            if tb % TPG == TPG - 1:
                reload_last_rows(tb // TPG)

        def regroup_relu_z(tb):
            cs = slice(P * tb, P * (tb + 1))
            if tb % TPG == 0:
                zg = zstage.tile([P, GW, 4], BF16, tag="zg", align_bytes=64)
                z_grouped[tb // TPG] = zg
            nc.vector.tensor_scalar(out=z_grouped[tb // TPG][:, P * (tb % TPG):P * (tb % TPG + 1), :],
                                    in0=z_raw[:, :, cs].rearrange("p t c -> p c t"),
                                    scalar1=floor[:, 0:1], scalar2=None, op0=ALU.max)

        def quantise_z(tb, tiles):
            cs = slice(P * tb, P * (tb + tiles))
            nc.vector.quantize_mx(out=zq[:, cs].bitcast(FP8X4), scales=zs[:, cs],
                                  in_=z_grouped[tb // TPG][:, P * (tb % TPG):P * (tb % TPG + tiles), :]
                                  .rearrange("p b t -> p (b t)"))

        def softmax_first():
            nc.vector.tensor_copy(out=t2f[:], in_=t2b[:])
            nc.vector.reciprocal(out=rinv[:], in_=t2f[:])
            nc.vector.tensor_scalar(out=lg[:], in0=ml_cols[:, :, 0:NT].rearrange("p e t -> p t e"),
                                    scalar1=rinv[:, 0:1], scalar2=-1.0, op0=ALU.mult, op1=ALU.mult)
            nc.vector.tensor_reduce(out=mx[:], in_=lg[:], axis=AX.X, op=ALU.max)
            nc.vector.tensor_tensor(out=lg[:], in0=lg[:], in1=mx[:].unsqueeze(2).to_broadcast([P, NT, E]),
                                    op=ALU.subtract)
            nc.scalar.activation(out=ex[:], in_=lg[:], func=ACT.Exp)

        def softmax_second():
            nc.vector.tensor_reduce(out=sm[:], in_=ex[:], axis=AX.X, op=ALU.add)
            nc.vector.reciprocal(out=rs[:], in_=sm[:])
            nc.vector.tensor_tensor(out=gate[:], in0=ex[:], in1=rs[:].unsqueeze(2).to_broadcast([P, NT, E]),
                                    op=ALU.mult)

        def gate_parts():
            nc.gpsimd.tensor_copy(out=gate_pad[:, :, 0:E], in_=gate[:])
            nc.gpsimd.tensor_tensor(out=gate_pad[:, :, E:2 * E], in0=gate[:], in1=gate_pad[:, :, 0:E],
                                    op=ALU.subtract)
            nc.gpsimd.tensor_scalar(out=g3m1[:], in0=gate[:, :, 3], scalar1=-1.0, scalar2=0.0, op0=ALU.add, op1=ALU.add)
            nc.gpsimd.tensor_copy(out=gate_pad[:, :, 8], in_=g3m1[:])
            nc.gpsimd.tensor_tensor(out=gate_pad[:, :, 9], in0=g3m1[:], in1=gate_pad[:, :, 8], op=ALU.subtract)

        ml_cols = bank([P, E, P], BF16)
        for e in range(E):
            nc.tensor.transpose(ml_cols[:, e, :], ml_rows[:].rearrange("t (p e) -> t e p", e=E)[:, e, :], ident_b[:])

        w_banks = {}
        w_grouped = {}

        def w_turn(e):
            w_grouped[e] = keep.tile([P, M, 4], BF16, name="wg%d" % e, align_bytes=64)
            for half in range(2):
                xt = bank([P, 2, 2, P], F32)
                for a in range(2):
                    words = w_raw[:, MT * e + 2 * half + a, :].bitcast(F32)
                    for u in range(2):
                        nc.tensor.transpose(xt[:, a, u, :], words[:, u:M // 2:2], ident_f[:])
                w_banks[(e, half)] = xt

        def w_exit(e, half, on_vector):
            dst = (w_grouped[e][:, 256 * half:256 * (half + 1), :].rearrange("p m j -> p (m j)").bitcast(F32)
                   .rearrange("p (a r u) -> p a r u", a=2, u=2))
            src = w_banks[(e, half)][:].rearrange("p a u r -> p a r u")
            if on_vector:
                nc.vector.tensor_copy(out=dst, in_=src)
            else:
                nc.scalar.copy(out=dst, in_=src)

        def w_quantise(e):
            nc.vector.quantize_mx(out=wq[:, e, :].bitcast(FP8X4), scales=ws[:, e, :],
                                  in_=w_grouped[e][:].rearrange("p m j -> p (m j)"))

        def gate_quarter(q):
            wt = bank([P, 8, P], BF16)
            for i in range(8):
                nc.tensor.transpose(wt[:, i, :], gate_pad[:, 8 * q + i, :], ident_b[:])
            rows = gate_rows[:, 1024 * q:1024 * (q + 1)]
            if q == 0:
                nc.vector.tensor_copy(out=rows, in_=wt[:].rearrange("p t c -> p (t c)"))
            else:
                nc.scalar.copy(out=rows, in_=wt[:].rearrange("p t c -> p (t c)"))

        nc.scalar.activation(out=z_last[:], in_=z_last[:], func=ACT.Relu)
        nc.scalar.dma_start(out=parked, in_=z_last[:])
        load_relu_rows(VECTOR_GROUPS)
        load_z(VECTOR_GROUPS)
        for g in range(VECTOR_GROUPS + 1, NG, 2):
            load_relu_rows(g, 2)
            load_z(g, 2)
        softmax_first()
        softmax_second()
        gate_parts()
        nc.gpsimd.tensor_copy(out=h_pad[:].rearrange("q (j r) -> q j r", j=MT),
                              in_=h_raw[:].rearrange("q (r j) -> q j r", j=MT))
        nc.gpsimd.tensor_copy(out=a_pad[:].rearrange("q (j r) -> q j r", j=MT),
                              in_=a_raw[:].rearrange("q (r j) -> q j r", j=MT))
        w_turn(0)
        w_turn(1)
        nc.vector.tensor_copy(out=h_f[:], in_=h_sb[:])
        nc.vector.tensor_tensor(out=dh_col[:], in0=h_f[:, 0:3, :],
                                in1=h_f[:, 3, :].unsqueeze(1).to_broadcast([P, E - 1, MT]), op=ALU.subtract)
        dh_banks = []
        for e in range(E - 1):
            db = bank([P, MT, P], F32)
            for j in range(MT):
                nc.tensor.transpose(db[:, j, :], dh_col[:, e, j:j + 1].to_broadcast([P, P]), ident_f[:])
            dh_banks.append(db)
        for e in range(2):
            w_exit(e, 0, False)
            w_exit(e, 1, False)
        w_turn(2)
        w_turn(3)
        for e in (0, 1):
            nc.scalar.copy(out=dh[:, e, :].rearrange("p (j r) -> p j r", j=MT), in_=dh_banks[e][:])
        w_quantise(0)
        regroup_relu_z(0)
        w_quantise(1)
        regroup_relu_z(1)
        regroup_relu_z(2)
        quantise_z(0, 2)
        regroup_relu_z(3)
        w_exit(2, 0, False)
        w_exit(2, 1, False)
        quantise_z(2, 2)
        w_exit(3, 0, False)
        w_exit(3, 1, False)
        for e in (2,):
            nc.scalar.copy(out=dh[:, e, :].rearrange("p (j r) -> p j r", j=MT), in_=dh_banks[e][:])
        w_quantise(2)
        w_quantise(3)

        off_tiles = [TPG * g + i for g in range(NG) for i in range(TPG - OFF_TILES[g], TPG)]
        product_fields = {}

        def h_product(tb, e):
            if e == 0:
                hf = products.tile([P, M], F32, tag="hf", bufs=H_BUFS)
                if tb < NT - 2 * TPG:
                    nc.gpsimd.tensor_scalar(out=hf[:], in0=dh[:, e, :], scalar1=gate[:, tb, e:e + 1], scalar2=0.0,
                                            op0=ALU.mult, op1=ALU.add)
                else:
                    nc.scalar.activation(out=hf[:], in_=dh[:, e, :], func=ACT.Copy, scale=gate[:, tb, e:e + 1])
                product_fields[tb] = [hf]
            else:
                pf = products.tile([P, M], F32, tag="pf")
                nc.scalar.activation(out=pf[:], in_=dh[:, e, :], func=ACT.Copy, scale=gate[:, tb, e:e + 1])
                hf = product_fields[tb][0]
                nc.gpsimd.tensor_tensor(out=hf[:], in0=hf[:], in1=pf[:], op=ALU.add)

        banks = {}
        tile_fields = {}
        g_banks = {}
        t_banks = {}
        gate_z = {}

        def mx_pass(tb, e):
            bs = slice(P * tb, P * (tb + 1))
            pe = bank([P, M], F32)
            nc.tensor.matmul_mx(out=pe[:], lhsT=zq[:, bs].bitcast(FP8X4), lhsT_scale=zs[:, bs],
                                rhs=wq[:, e, :].bitcast(FP8X4), rhs_scale=ws[:, e, :],
                                start=True, stop=True)
            banks[(tb, e)] = pe

        def scalar_exit(tb, e):
            fld = fields.tile([P, M], F32, tag="f%d" % e)
            nc.scalar.activation(out=fld[:], in_=banks[(tb, e)][:], func=ACT.Copy, scale=gate[:, tb, e:e + 1])
            tile_fields[tb] = tile_fields.get(tb, []) + [fld]

        def vector_exit(tb, e):
            fld = tile_fields[tb][e - 2]
            nc.vector.scalar_tensor_tensor(out=fld[:], in0=banks[(tb, e)][:], scalar=gate[:, tb, e:e + 1],
                                           in1=fld[:], op0=ALU.mult, op1=ALU.add)

        def sum_fields(tb):
            f0, f1 = tile_fields[tb]
            nc.gpsimd.tensor_tensor(out=f0[:], in0=f0[:], in1=f1[:], op=ALU.add)
            tile_fields[tb] = [f0]

        def gate_a(u):
            g, mt = u // MT, u % MT
            b2 = bank([P, GW], F32)
            nc.tensor.matmul(out=b2[:], lhsT=a_pad[:, P * mt:P * (mt + 1)], rhs=gate_rows[:, GW * g:GW * (g + 1)],
                             start=True, stop=True)
            g_banks[u] = b2

        def turned_sum(u):
            g, mt = u // MT, u % MT
            ms = slice(P * mt, P * (mt + 1))
            wide = GW - P * OFF_TILES[g]
            todo = [(i, fld) for i in range(TPG)
                    for fld in tile_fields[TPG * g + i] + product_fields.get(TPG * g + i, [])]
            b1 = bank([P, GW], F32)
            nc.tensor.matmul(out=b1[:, 0:wide], lhsT=h_pad[:, ms],
                             rhs=gate_rows[:, GW * g:GW * g + wide], start=True, stop=False)
            for n, (i, fld) in enumerate(todo):
                nc.tensor.matmul(out=b1[:, P * i:P * (i + 1)], lhsT=fld[:, ms], rhs=ident_f[:],
                                 is_transpose=True, start=False, stop=(n == len(todo) - 1))
            t_banks[u] = b1

        def times_z(u):
            g, mt = u // MT, u % MT
            gz = outs.tile([P, GW], F32, tag="gz", bufs=GZ_BUFS)
            nc.vector.tensor_tensor(out=gz[:], in0=g_banks[u][:],
                                    in1=z_raw[:, mt, GW * g:GW * (g + 1)], op=ALU.mult)
            gate_z[u] = gz

        def last_add(u):
            g, mt = u // MT, u % MT
            xs = outs.tile([P, GW], F32, tag="xs")
            nc.vector.scalar_tensor_tensor(out=xs[:], in0=t_banks[u][:], scalar=h_f[:, 3, mt:mt + 1],
                                           in1=gate_z[u][:], op0=ALU.add, op1=ALU.add)
            nc.sync.dma_start(out=out_view[:, mt, GW * g:GW * (g + 1)], in_=xs[:])

        UNITS = NG * MT
        regrouped = [TPG * VECTOR_GROUPS - 1]
        for s in range(-1, NT + LAG + 1):
            u = s - LAG
            if 0 <= u + 1 < UNITS:
                gate_a(u + 1)
            if s + 1 < NT:
                mx_pass(s + 1, 0)
                mx_pass(s + 1, 1)
            if 0 <= s < NT:
                mx_pass(s, 2)
                mx_pass(s, 3)
            if 0 <= u < UNITS:
                turned_sum(u)
            if s + 1 < NT:
                scalar_exit(s + 1, 0)
                scalar_exit(s + 1, 1)
            if 0 < s < NT:
                for n in range(products_by(s - 1), min(products_by(s), (E - 1) * len(off_tiles))):
                    h_product(off_tiles[n // (E - 1)], n % (E - 1))
            while regrouped[0] < min(NT - 1, s + AHEAD_COPY, 2 * s + 9):
                regrouped[0] += 1
                regroup_z(regrouped[0])
            if s < 2 * VECTOR_GROUPS - 3:
                regroup_relu_z(2 * s + 6)
                regroup_relu_z(2 * s + 7)
            if 0 <= u + 1 < UNITS:
                times_z(u + 1)
            if 0 <= u - 1 < UNITS:
                last_add(u - 1)
            if s > 0 and (s + QLEAD) % TPG == 0 and s + QLEAD < NT:
                quantise_z(s + QLEAD, TPG)
            if 0 <= s < NT:
                vector_exit(s, 2)
                vector_exit(s, 3)
                if s % TPG < 2 and s < NT - TPG:
                    sum_fields(s)
            if s == 0 or s > 0 and (s + 2) % (2 * TPG) == 0 and s + 2 < NT:
                gate_quarter((s + 2) // (2 * TPG))
